import numpy as np
import ml_dtypes


def mxq(x, axis, fmt="e4m3"):
    dtype, down = {"e4m3": (ml_dtypes.float8_e4m3fn, 7), "e5m2": (ml_dtypes.float8_e5m2, 14)}[fmt]
    v = np.moveaxis(np.asarray(x, np.float32).astype(ml_dtypes.bfloat16).astype(np.float64), axis, -1)
    blocks = v.reshape(v.shape[:-1] + (-1, 32))
    amax = np.abs(blocks).max(-1, keepdims=True)
    byte = np.maximum(np.where(amax > 0, np.frexp(amax)[1] - 1 + 127, 0) - down, 1)
    scale = np.exp2(byte - 127.0)
    codes = (blocks / scale).astype(np.float32).astype(dtype).astype(np.float64)
    return np.moveaxis((codes * scale).reshape(v.shape), -1, axis)


WIDE = False


def mx_kscale(k):
    if not WIDE:
        return np.ones(k)
    levels = np.array([10, -10, 5, -5, 0])
    a = np.random.permutation(np.resize(levels, k // 512 * 4)).reshape(k // 512, 4)
    idx = np.arange(k)
    return np.exp2(a[idx // 512, idx % 128 // 32])


BF16 = ml_dtypes.bfloat16


def bf(x):
    return np.asarray(x, np.float32).astype(BF16)


def f64(x):
    return np.asarray(x).astype(np.float64)


B, K, F, INCH, OUTCH, R = 2, 4, 128, 2048, 2048, 128


def erf(a):
    c = np.clip(a, -6.0, 6.0)
    c2 = 2.0 * c * c
    t = c.copy()
    s = c.copy()
    n = 1.0
    while np.max(np.abs(t) - 1e-18 * np.abs(s)) > 0.0:
        n += 2.0
        t = t * c2 / n
        s = s + t
    return 2.0 / np.sqrt(np.pi) * np.exp(-c * c) * s


def gelu(t):
    return 0.5 * t * (1.0 + erf(t / np.sqrt(2.0)))


def setup_inputs():
    s = mx_kscale(INCH)
    return {
        "h": bf(gelu(np.random.standard_normal((B, K, F, INCH))) * s),
        "z": bf(np.random.standard_normal((B, K, F, R)) * 0.35),
        "u": bf(np.random.standard_normal((B, K, OUTCH, R)) * 1.5 * np.sqrt(R)),
        "b": bf(np.random.standard_normal((B, 1, 1, OUTCH)) * 0.3),
        "W_out": bf(np.random.standard_normal((OUTCH, INCH)) * 1.5 / np.sqrt(INCH) / s),
        "b_out": bf(np.random.standard_normal(OUTCH) * 0.3),
    }


def reference(h, z, u, b, W_out, b_out):
    lora = f64(z) @ f64(u).transpose(0, 1, 3, 2) / R
    main = mxq(f64(h), 3, "e4m3") @ mxq(f64(W_out).T, 0, "e4m3")
    return gelu(main + f64(b_out) + lora + f64(b))

@@ -1,0 +1,320 @@
+from contextlib import ExitStack
+
+import concourse.mybir as mybir
+from concourse.masks import make_identity
+
+F32 = mybir.dt.float32
+BF16 = mybir.dt.bfloat16
+U32 = mybir.dt.uint32
+U8 = mybir.dt.uint8
+I32 = mybir.dt.int32
+FP8X4 = mybir.dt.float8_e4m3fn_x4
+GELU = mybir.ActivationFunctionType.Gelu
+MULT = mybir.AluOpType.mult
+ADD = mybir.AluOpType.add
+
+P = 128
+GROUPS = 8
+CHUNKS = 4
+PASSES = 4
+NCOL = 512
+KDIM = 2048
+ODIM = 2048
+RANK = 128
+FLOPS = 2 * GROUPS * P * ODIM * (KDIM + RANK)
+
+VEC_BLOCKS = {0: (0, 2), 2: (0,), 4: (0,), 5: (0,)}
+
+
+def tile_loratacmlp4_pb_kernel(tc, h, z, u, b, W_out, b_out, out):
+    nc = tc.nc
+    h_v = h.rearrange("b k f c -> (b k) f c")
+    w_v = W_out.rearrange("(c p t) k -> c p t k", p=P, t=4)
+    u_v = u.rearrange("b k (c p t) r -> c p (b k) (t r)", p=P, t=4)
+    z_v = z.rearrange("b k f r -> f (b k) r")
+    b_v = b.rearrange("b x y o -> (b x y) o")
+    bo_v = b_out.rearrange("(x o) -> x o", x=1)
+    out_v = out.rearrange("b k f o -> f (b k) o")
+
+    units_of = [[g] for g in range(GROUPS)]
+    for c in range(1, CHUNKS):
+        for g in range(0, GROUPS, 2):
+            units_of.append([GROUPS * c + g, GROUPS * c + g + 1])
+    n_steps = len(units_of)
+
+    blocks_at = {}
+    for k in range(n_steps):
+        blocks_at[k] = []
+    blocks_at[0] = [("h", 1, 0, 0), ("h", 1, 0, 1), ("h", 2, 0, 0), ("h", 2, 0, 1)]
+    for g in range(3, GROUPS):
+        blocks_at[g - 2] = [("h", g, 0, 0), ("h", g, 0, 1)]
+    for k, kp, j in ((1, 0, 0), (2, 0, 1), (3, 1, 0), (4, 1, 1), (5, 2, 0), (5, 2, 1), (6, 3, 0), (6, 3, 1)):
+        blocks_at[k].append(("w", 1, kp, j))
+    for c in (2, 3):
+        for kp in range(PASSES):
+            blocks_at[4 * c - 1 + kp].extend([("w", c, kp, 0), ("w", c, kp, 1)])
+    front_at = {0: 2}
+
+    with ExitStack() as ctx:
+        const = ctx.enter_context(tc.tile_pool(name="const", bufs=1))
+        hraw_pool = ctx.enter_context(tc.tile_pool(name="hraw", bufs=4))
+        wraw_pool = ctx.enter_context(tc.tile_pool(name="wraw", bufs=3))
+        uraw_pool = ctx.enter_context(tc.tile_pool(name="uraw", bufs=3))
+        ut_pool = ctx.enter_context(tc.tile_pool(name="ut", bufs=3))
+        grp_pool = ctx.enter_context(tc.tile_pool(name="grouped", bufs=4))
+        wq_pool = ctx.enter_context(tc.tile_pool(name="wq", bufs=2))
+        l_pool = ctx.enter_context(tc.tile_pool(name="lsum", bufs=4))
+        o_pool = ctx.enter_context(tc.tile_pool(name="res", bufs=4))
+        ps_mm = ctx.enter_context(tc.psum_pool(name="ps_mm", bufs=2))
+        ps_lo = ctx.enter_context(tc.psum_pool(name="ps_lo", bufs=2))
+        ps_tw = ctx.enter_context(tc.psum_pool(name="ps_tw", bufs=3))
+        ps_tu = ctx.enter_context(tc.psum_pool(name="ps_tu", bufs=1))
+        ctx.enter_context(tc.manual_schedule())
+
+        hraw = {}
+        wraw = {}
+        uraw = {}
+        ut = {}
+        grouped = {}
+        wcodes = {}
+        wscales = {}
+        lora_ps = {}
+        lsum = {}
+        main = {}
+        res = {}
+        pending = []
+        done = [0]
+
+        ident_f = const.tile([P, P], F32, name="ident_f")
+        ident_b = const.tile([P, P], BF16, name="ident_b")
+        rows = const.tile([P, ODIM], BF16, name="rows")
+        sel = [const.tile([P, P], BF16, name="sel%d" % i) for i in range(2)]
+        bias = const.tile([P, 2, ODIM], F32, name="bias")
+        zraw = const.tile([P, GROUPS, RANK], BF16, name="zraw")
+        z_t = const.tile([P, GROUPS, P], BF16, name="z_t")
+        hcodes = const.tile([P, GROUPS, PASSES * P], U32, name="hcodes", align_bytes=64)
+        hscales = const.tile([P, GROUPS, PASSES * P], U8, name="hscales", align_bytes=64)
+
+        def load_h(g):
+            hraw[g] = hraw_pool.tile([P, KDIM], BF16, name="hraw%d" % g, tag="hraw")
+            nc.sync.dma_start(out=hraw[g][:], in_=h_v[g])
+
+        def load_w(c, k0, k1):
+            t = wraw_pool.tile([P, 4, 512 * (k1 - k0)], BF16, name="wraw%d_%d" % (c, k0), tag="wraw%d" % (k1 - k0),
+                               bufs=(8 if k1 - k0 == 1 else 2))
+            nc.sync.dma_start(out=t[:], in_=w_v[c][:, :, 512 * k0:512 * k1])
+            for kp in range(k0, k1):
+                wraw[(c, kp)] = (t, kp - k0)
+
+        def load_u(c, g0, g1):
+            if c not in uraw:
+                uraw[c] = uraw_pool.tile([P, GROUPS, NCOL], BF16, name="uraw%d" % c, tag="uraw")
+            nc.sync.dma_start(out=uraw[c][:, g0:g1, :], in_=u_v[c][:, g0:g1, :])
+
+        def copy_out(on_vector, dst, src):
+            if on_vector:
+                nc.vector.tensor_copy(out=dst, in_=src)
+            else:
+                nc.scalar.copy(out=dst, in_=src)
+
+        def block(blk, on_vector):
+            kind, a0, kp0, j = blk
+            key = (kind, a0, kp0)
+            if key not in grouped:
+                grouped[key] = grp_pool.tile([P, 4 * NCOL], BF16, name="grp_%s%d_%d" % key, tag="grp", align_bytes=64)
+            ps = ps_tw.tile([P, 2, 2, P], F32, name="tw_%s%d_%d_%d" % blk, tag="tw")
+            for a in range(2):
+                for v in range(2):
+                    if kind == "h":
+                        w0 = 256 * (2 * j + a) + 128 * v
+                        src = hraw[a0][:].bitcast(F32)[:, w0:w0 + 128]
+                    else:
+                        wt, kl = wraw[(a0, kp0)]
+                        w0 = 256 * kl + 128 * v
+                        src = wt[:, 2 * j + a, :].bitcast(F32)[:, w0:w0 + 128]
+                    nc.tensor.transpose(ps[:, a, v, :], src, ident_f[:])
+            dst = grouped[key][:].bitcast(F32).rearrange("q (a r v) -> q a r v", a=4, v=2)
+            copy_out(on_vector, dst[:, 2 * j:2 * j + 2, :, :], ps[:].rearrange("q a v r -> q a r v"))
+            if j == 1:
+                pending.append(key)
+
+        def quantise(key):
+            kind, a0, kp0 = key
+            if kind == "h":
+                codes = hcodes[:, a0, :]
+                scales = hscales[:, a0, :]
+            else:
+                if a0 not in wcodes:
+                    wcodes[a0] = wq_pool.tile([P, PASSES, NCOL], U32, name="wcodes%d" % a0, tag="wcodes", align_bytes=64)
+                    wscales[a0] = wq_pool.tile([P, PASSES, NCOL], U8, name="wscales%d" % a0, tag="wscales", align_bytes=64)
+                codes = wcodes[a0][:, kp0, :]
+                scales = wscales[a0][:, kp0, :]
+            nc.vector.quantize_mx(out=codes.bitcast(FP8X4), scales=scales, in_=grouped[key][:])
+
+        def flush(keep):
+            while len(pending) - done[0] > keep:
+                quantise(pending[done[0]])
+                done[0] = done[0] + 1
+
+        def mx(n):
+            c, g = divmod(n, GROUPS)
+            main[n] = ps_mm.tile([P, NCOL], F32, name="acc%d" % n, tag="acc")
+            for kp in range(PASSES):
+                nc.tensor.matmul_mx(
+                    out=main[n][:],
+                    lhsT=hcodes[:, g, P * kp:P * kp + P].bitcast(FP8X4),
+                    lhsT_scale=hscales[:, g, P * kp:P * kp + P],
+                    rhs=wcodes[c][:, kp, :].bitcast(FP8X4),
+                    rhs_scale=wscales[c][:, kp, :],
+                    start=(kp == 0),
+                    stop=(kp == PASSES - 1),
+                )
+
+        def by_column(ap):
+            return ap.rearrange("q (p t) -> q p t", t=4)
+
+        def by_plane(ap):
+            return ap.rearrange("q (t p) -> q p t", t=4)
+
+        def add_main(n, dst):
+            nc.vector.tensor_tensor(out=by_column(dst), in0=by_plane(main[n][:]), in1=by_column(lsum[n][:]), op=ADD)
+
+        def lora_mm(n, rhs):
+            g = n % GROUPS
+            lora_ps[n] = ps_lo.tile([P, NCOL], F32, name="lo%d" % n, tag="lo")
+            nc.tensor.matmul(out=lora_ps[n][:], lhsT=z_t[:, g, :], rhs=rhs, start=True, stop=True)
+
+        def lora_out(n):
+            c, g = divmod(n, GROUPS)
+            lsum[n] = l_pool.tile([P, NCOL], F32, name="lsum%d" % n, tag="lsum")
+            nc.vector.scalar_tensor_tensor(
+                out=by_column(lsum[n][:]),
+                in0=by_plane(lora_ps[n][:]),
+                scalar=1.0 / RANK,
+                in1=by_column(bias[:, g // 4, NCOL * c:NCOL * c + NCOL]),
+                op0=MULT,
+                op1=ADD,
+            )
+
+        def units(k):
+            if 0 <= k < n_steps:
+                return units_of[k]
+            return []
+
+        def plain(k):
+            blks = blocks_at.get(k, [])
+            vec = VEC_BLOCKS.get(k, ())
+            front = front_at.get(k, 0)
+            for i in range(front):
+                block(blks[i], i in vec)
+            nxt = units(k + 1)
+            nxt2 = units(k + 2)
+            tu = None
+            if nxt2:
+                tu = ps_tu.tile([P, len(nxt2), 4, P], BF16, name="tu%d" % (k + 2), tag="tu")
+            for i in range(max(len(nxt), len(nxt2))):
+                if i < len(nxt):
+                    lora_mm(nxt[i], ut[k + 1][:, i, :])
+                if i < len(nxt2):
+                    c, g = divmod(nxt2[i], GROUPS)
+                    for t in range(4):
+                        nc.tensor.transpose(tu[:, i, t, :], uraw[c][:, g, P * t:P * t + P], ident_b[:])
+            if nxt2:
+                ut[k + 2] = ut_pool.tile([P, len(nxt2), NCOL], BF16, name="ut%d" % (k + 2), tag="ut")
+                nc.scalar.copy(out=ut[k + 2][:], in_=tu[:].rearrange("q i t p -> q i (t p)"))
+            for n in nxt:
+                lora_out(n)
+            for i in range(front, len(blks)):
+                block(blks[i], i in vec)
+
+        def finish(k, i0, i1):
+            c, g = divmod(units_of[k][i0], GROUPS)
+            nc.scalar.activation(out=res[k][:, i0:i1, :], in_=res[k][:, i0:i1, :], func=GELU)
+            nc.sync.dma_start(out=out_v[:, g:g + i1 - i0, NCOL * c:NCOL * c + NCOL], in_=res[k][:, i0:i1, :])
+
+        loads_at = {
+            0: [("h", 5), ("h", 6), ("w", 1, 2, 3)],
+            1: [("h", 7), ("w", 1, 3, 4)],
+            2: [("u", 1, 0, 8)],
+            3: [("w", 2, 0, 4)],
+            4: [("u", 2, 0, 8)],
+            5: [("w", 3, 0, 4)],
+            6: [("u", 3, 0, 8)],
+        }
+
+        def do_load(item):
+            if item[0] == "h":
+                load_h(item[1])
+            elif item[0] == "w":
+                load_w(item[1], item[2], item[3])
+            else:
+                load_u(item[1], item[2], item[3])
+
+        warm = const.tile([P, 8], F32, name="warm")
+        nc.vector.memset(warm[:], 0.0)
+        nc.scalar.activation(out=warm[:], in_=warm[:], func=GELU)
+        nc.vector.memset(rows[:].bitcast(I32), 0)
+        nc.sync.dma_start(out=rows[0:1, :], in_=bo_v)
+        nc.sync.dma_start(out=rows[32:33, :], in_=b_v[0:1, :])
+        nc.sync.dma_start(out=rows[64:65, :], in_=b_v[1:2, :])
+        nc.sync.dma_start(out=zraw[:], in_=z_v)
+        load_u(0, 0, 4)
+        load_h(0)
+        for kp in range(PASSES):
+            load_w(0, kp, kp + 1)
+        load_h(1)
+        load_h(2)
+        load_w(1, 0, 1)
+        load_h(3)
+        make_identity(nc, ident_b[:])
+        make_identity(nc, ident_f[:])
+        for i in range(2):
+            nc.vector.memset(sel[i][:], 0.0)
+            nc.vector.memset(sel[i][0:1, :], 1.0)
+            nc.vector.memset(sel[i][32 * (i + 1):32 * (i + 1) + 1, :], 1.0)
+
+        def bias_mm(i):
+            bb, c = divmod(i, CHUNKS)
+            if i % 2 == 0:
+                ps = ps_mm.tile([P, NCOL], F32, name="bias_ps%d" % i, tag="acc")
+            else:
+                ps = ps_lo.tile([P, NCOL], F32, name="bias_ps%d" % i, tag="lo")
+            nc.tensor.matmul(out=ps[:], lhsT=sel[bb][:], rhs=rows[:, NCOL * c:NCOL * c + NCOL], start=True, stop=True)
+            copy_out(i % 2 == 0, bias[:, bb, NCOL * c:NCOL * c + NCOL], ps[:])
+
+        for i in range(4):
+            bias_mm(i)
+        tz = ps_tu.tile([P, GROUPS, P], BF16, name="tz", tag="tu")
+        for g in range(GROUPS):
+            nc.tensor.transpose(tz[:, g, :], zraw[:, g, :], ident_b[:])
+        nc.scalar.copy(out=z_t[:], in_=tz[:])
+        plain(-2)
+        for i in range(4, 8):
+            bias_mm(i)
+        plain(-1)
+        block(("h", 0, 0, 0), True)
+        block(("h", 0, 0, 1), False)
+        for kp in range(PASSES):
+            block(("w", 0, kp, 0), True)
+            block(("w", 0, kp, 1), False)
+            flush(1)
+        load_h(4)
+        load_u(0, 4, 8)
+        load_w(1, 1, 2)
+
+        for k in range(n_steps):
+            flush(0)
+            us = units_of[k]
+            res[k] = o_pool.tile([P, len(us), NCOL], F32, name="res%d" % k, tag="res")
+            for n in us:
+                mx(n)
+            for i in range(len(us)):
+                add_main(us[i], res[k][:, i, :])
+            plain(k)
+            for item in loads_at.get(k, []):
+                do_load(item)
+            if k == n_steps - 1:
+                for i in range(len(us)):
+                    finish(k, i, i + 1)
+            else:
+                finish(k, 0, len(us))

@@ -23,7 +23,106 @@ ODIM = 2048
 RANK = 128
 FLOPS = 2 * GROUPS * P * ODIM * (KDIM + RANK)
 
-VEC_BLOCKS = {0: (0, 2), 2: (0,), 4: (0,), 5: (0,)}
+LATE_STEP = 2
+LEAD = 6
+VEC_BLK = {1: (0,), 3: (0,), 4: (0,)}
+W1_AT = ((1, 0, 0), (2, 0, 1), (3, 1, 0), (3, 1, 1), (4, 2, 0), (4, 2, 1), (5, 3, 0), (6, 3, 1))
+
+
+def build_program():
+    units_of = [[g] for g in range(GROUPS)]
+    for c in range(1, CHUNKS):
+        for g in range(0, GROUPS, LATE_STEP):
+            units_of.append([GROUPS * c + g + i for i in range(LATE_STEP)])
+    n_steps = len(units_of)
+    n_units = GROUPS * CHUNKS
+
+    def ahead(k):
+        if 0 <= k < n_steps:
+            return [n + LEAD for n in units_of[k] if n + LEAD < n_units]
+        return []
+
+    blocks_at = {}
+    for k in range(n_steps):
+        blocks_at[k] = []
+    for g in range(2, GROUPS):
+        blocks_at[g - 2] = [("h", g, 0, 0), ("h", g, 0, 1)]
+    for k, kp, j in W1_AT:
+        blocks_at[k].append(("w", 1, kp, j))
+    for c in (2, 3):
+        for kp in range(PASSES):
+            blocks_at[4 * c - 1 + kp].extend([("w", c, kp, 0), ("w", c, kp, 1)])
+
+    loads_at = {
+        0: [("h", 6), ("w", 1, 2, 3)],
+        1: [("h", 7), ("w", 1, 3, 4)],
+        2: [("u", 2, 0, 8)],
+        3: [("w", 2, 0, 1), ("w", 2, 1, 2)],
+        4: [("w", 2, 2, 3), ("w", 2, 3, 4)],
+        5: [("u", 3, 0, 8)],
+        7: [("w", 3, 0, 1), ("w", 3, 1, 2)],
+        8: [("w", 3, 2, 3), ("w", 3, 3, 4)],
+    }
+
+    head = []
+    for item in (("z",), ("u", 0, 0, 4), ("u", 0, 4, 8), ("h", 0), ("w", 0, 0, 1), ("w", 0, 1, 2), ("w", 0, 2, 3),
+                 ("w", 0, 3, 4), ("h", 1), ("u", 1, 0, 4), ("h", 2), ("h", 3), ("w", 1, 0, 1)):
+        head.append(("load", item))
+
+    def lora(n):
+        return [("mm", n, 0, NCOL), ("lout", n)]
+
+    head.extend([("bias", 0, True), ("bias", 1, False), ("bias", 2, True), ("bias", 3, False), ("zt",)])
+    head.extend([("bias", 4, True), ("ut", [0, 1], "tu"), ("ut", [2, 3], "tu"), ("bias", 5, False)])
+    head.extend(lora(0) + lora(1) + [("ut", [4, 5], "tu")] + lora(2) + lora(3) + [("ut", [6, 7], "tu")])
+    head.extend([("blk", ("h", 0, 0, 0), False), ("blk", ("h", 0, 0, 1), False), ("load", ("h", 4))])
+    head.extend(lora(4))
+    head.extend([("blk", ("w", 0, 0, 0), False), ("blk", ("w", 0, 0, 1), False), ("flush", 1)])
+    head.extend(lora(5))
+    head.extend([("blk", ("w", 0, 1, 0), False), ("blk", ("w", 0, 1, 1), False), ("flush", 1)])
+    head.extend(lora(6))
+    head.extend([("blk", ("w", 0, 2, 0), False), ("blk", ("w", 0, 2, 1), False), ("flush", 1)])
+    head.extend([("bias", 6, True)])
+    head.extend([("blk", ("w", 0, 3, 0), True), ("blk", ("w", 0, 3, 1), False), ("flush", 0)])
+    head.extend([("bias", 7, True)])
+    head.extend([("blk", ("h", 1, 0, 0), True), ("blk", ("h", 1, 0, 1), False)])
+    head.extend([("load", ("h", 5)), ("load", ("w", 1, 1, 2)), ("load", ("u", 1, 4, 8))])
+
+    steps = []
+    for k in range(n_steps):
+        ops = []
+        us = units_of[k]
+        vec = VEC_BLK.get(k, ())
+        blks = [("blk", blk, i in vec) for i, blk in enumerate(blocks_at[k])]
+        if len(us) == 1:
+            ops.append(("flush", 0))
+            ops.append(("add", us[0], 0))
+        else:
+            ops.append(("add", us[0], 0))
+            ops.append(("flush", 0))
+            ops.append(("add", us[1], 1))
+        nxt = ahead(k + 1)
+        nxt2 = ahead(k + 2)
+        last = []
+        if len(nxt) == 1:
+            ops.append(("mm", nxt[0], 0, NCOL // 2))
+            last = [("mm", nxt[0], NCOL // 2, NCOL), ("lout", nxt[0])]
+        elif len(nxt) == 2:
+            ops.extend(lora(nxt[0]))
+            last = lora(nxt[1])
+        if nxt2:
+            ops.append(("ut", nxt2, "tu"))
+        ops.extend(blks)
+        ops.extend(last)
+        for item in loads_at.get(k, []):
+            ops.append(("load", item))
+        if k == n_steps - 1:
+            for i in range(len(us)):
+                ops.append(("fin", i, i + 1))
+        else:
+            ops.append(("fin", 0, len(us)))
+        steps.append((us, ops))
+    return head, steps
 
 
 def tile_loratacmlp4_pb_kernel(tc, h, z, u, b, W_out, b_out, out):
@@ -36,39 +135,19 @@ def tile_loratacmlp4_pb_kernel(tc, h, z, u, b, W_out, b_out, out):
     bo_v = b_out.rearrange("(x o) -> x o", x=1)
     out_v = out.rearrange("b k f o -> f (b k) o")
 
-    units_of = [[g] for g in range(GROUPS)]
-    for c in range(1, CHUNKS):
-        for g in range(0, GROUPS, 2):
-            units_of.append([GROUPS * c + g, GROUPS * c + g + 1])
-    n_steps = len(units_of)
-
-    blocks_at = {}
-    for k in range(n_steps):
-        blocks_at[k] = []
-    blocks_at[0] = [("h", 1, 0, 0), ("h", 1, 0, 1), ("h", 2, 0, 0), ("h", 2, 0, 1)]
-    for g in range(3, GROUPS):
-        blocks_at[g - 2] = [("h", g, 0, 0), ("h", g, 0, 1)]
-    for k, kp, j in ((1, 0, 0), (2, 0, 1), (3, 1, 0), (4, 1, 1), (5, 2, 0), (5, 2, 1), (6, 3, 0), (6, 3, 1)):
-        blocks_at[k].append(("w", 1, kp, j))
-    for c in (2, 3):
-        for kp in range(PASSES):
-            blocks_at[4 * c - 1 + kp].extend([("w", c, kp, 0), ("w", c, kp, 1)])
-    front_at = {0: 2}
+    head, steps = build_program()
 
     with ExitStack() as ctx:
         const = ctx.enter_context(tc.tile_pool(name="const", bufs=1))
         hraw_pool = ctx.enter_context(tc.tile_pool(name="hraw", bufs=4))
-        wraw_pool = ctx.enter_context(tc.tile_pool(name="wraw", bufs=3))
+        wraw_pool = ctx.enter_context(tc.tile_pool(name="wraw", bufs=8))
         uraw_pool = ctx.enter_context(tc.tile_pool(name="uraw", bufs=3))
         ut_pool = ctx.enter_context(tc.tile_pool(name="ut", bufs=3))
         grp_pool = ctx.enter_context(tc.tile_pool(name="grouped", bufs=4))
         wq_pool = ctx.enter_context(tc.tile_pool(name="wq", bufs=2))
-        l_pool = ctx.enter_context(tc.tile_pool(name="lsum", bufs=4))
-        o_pool = ctx.enter_context(tc.tile_pool(name="res", bufs=4))
-        ps_mm = ctx.enter_context(tc.psum_pool(name="ps_mm", bufs=2))
-        ps_lo = ctx.enter_context(tc.psum_pool(name="ps_lo", bufs=2))
-        ps_tw = ctx.enter_context(tc.psum_pool(name="ps_tw", bufs=3))
-        ps_tu = ctx.enter_context(tc.psum_pool(name="ps_tu", bufs=1))
+        l_pool = ctx.enter_context(tc.tile_pool(name="lsum", bufs=LEAD + 3))
+        o_pool = ctx.enter_context(tc.tile_pool(name="res", bufs=5))
+        psum = ctx.enter_context(tc.psum_pool(name="psum", bufs=8))
         ctx.enter_context(tc.manual_schedule())
 
         hraw = {}
@@ -81,7 +160,6 @@ def tile_loratacmlp4_pb_kernel(tc, h, z, u, b, W_out, b_out, out):
         lora_ps = {}
         lsum = {}
         main = {}
-        res = {}
         pending = []
         done = [0]
 
@@ -94,14 +172,14 @@ def tile_loratacmlp4_pb_kernel(tc, h, z, u, b, W_out, b_out, out):
         z_t = const.tile([P, GROUPS, P], BF16, name="z_t")
         hcodes = const.tile([P, GROUPS, PASSES * P], U32, name="hcodes", align_bytes=64)
         hscales = const.tile([P, GROUPS, PASSES * P], U8, name="hscales", align_bytes=64)
+        warm = const.tile([P, 8], F32, name="warm")
 
         def load_h(g):
             hraw[g] = hraw_pool.tile([P, KDIM], BF16, name="hraw%d" % g, tag="hraw")
             nc.sync.dma_start(out=hraw[g][:], in_=h_v[g])
 
         def load_w(c, k0, k1):
-            t = wraw_pool.tile([P, 4, 512 * (k1 - k0)], BF16, name="wraw%d_%d" % (c, k0), tag="wraw%d" % (k1 - k0),
-                               bufs=(8 if k1 - k0 == 1 else 2))
+            t = wraw_pool.tile([P, 4, 512 * (k1 - k0)], BF16, name="wraw%d_%d" % (c, k0), tag="wraw")
             nc.sync.dma_start(out=t[:], in_=w_v[c][:, :, 512 * k0:512 * k1])
             for kp in range(k0, k1):
                 wraw[(c, kp)] = (t, kp - k0)
@@ -110,6 +188,16 @@ def tile_loratacmlp4_pb_kernel(tc, h, z, u, b, W_out, b_out, out):
             if c not in uraw:
                 uraw[c] = uraw_pool.tile([P, GROUPS, NCOL], BF16, name="uraw%d" % c, tag="uraw")
             nc.sync.dma_start(out=uraw[c][:, g0:g1, :], in_=u_v[c][:, g0:g1, :])
+
+        def do_load(item):
+            if item[0] == "z":
+                nc.sync.dma_start(out=zraw[:], in_=z_v)
+            elif item[0] == "h":
+                load_h(item[1])
+            elif item[0] == "w":
+                load_w(item[1], item[2], item[3])
+            else:
+                load_u(item[1], item[2], item[3])
 
         def copy_out(on_vector, dst, src):
             if on_vector:
@@ -122,7 +210,7 @@ def tile_loratacmlp4_pb_kernel(tc, h, z, u, b, W_out, b_out, out):
             key = (kind, a0, kp0)
             if key not in grouped:
                 grouped[key] = grp_pool.tile([P, 4 * NCOL], BF16, name="grp_%s%d_%d" % key, tag="grp", align_bytes=64)
-            ps = ps_tw.tile([P, 2, 2, P], F32, name="tw_%s%d_%d_%d" % blk, tag="tw")
+            ps = psum.tile([P, 2, 2, P], F32, name="tw_%s%d_%d_%d" % blk, tag="bank")
             for a in range(2):
                 for v in range(2):
                     if kind == "h":
@@ -158,7 +246,7 @@ def tile_loratacmlp4_pb_kernel(tc, h, z, u, b, W_out, b_out, out):
 
         def mx(n):
             c, g = divmod(n, GROUPS)
-            main[n] = ps_mm.tile([P, NCOL], F32, name="acc%d" % n, tag="acc")
+            main[n] = psum.tile([P, NCOL], F32, name="acc%d" % n, tag="bank")
             for kp in range(PASSES):
                 nc.tensor.matmul_mx(
                     out=main[n][:],
@@ -179,10 +267,22 @@ def tile_loratacmlp4_pb_kernel(tc, h, z, u, b, W_out, b_out, out):
         def add_main(n, dst):
             nc.vector.tensor_tensor(out=by_column(dst), in0=by_plane(main[n][:]), in1=by_column(lsum[n][:]), op=ADD)
 
-        def lora_mm(n, rhs):
+        def u_transposes(us, tag):
+            tu = psum.tile([P, len(us), 4, P], BF16, name="tu%d" % us[0], tag="bank")
+            for i in range(len(us)):
+                c, g = divmod(us[i], GROUPS)
+                for t in range(4):
+                    nc.tensor.transpose(tu[:, i, t, :], uraw[c][:, g, P * t:P * t + P], ident_b[:])
+            t_sb = ut_pool.tile([P, len(us), NCOL], BF16, name="ut%d" % us[0], tag="ut")
+            nc.scalar.copy(out=t_sb[:], in_=tu[:].rearrange("q i t p -> q i (t p)"))
+            for i in range(len(us)):
+                ut[us[i]] = t_sb[:, i, :]
+
+        def lora_mm(n, c0, c1):
             g = n % GROUPS
-            lora_ps[n] = ps_lo.tile([P, NCOL], F32, name="lo%d" % n, tag="lo")
-            nc.tensor.matmul(out=lora_ps[n][:], lhsT=z_t[:, g, :], rhs=rhs, start=True, stop=True)
+            if c0 == 0:
+                lora_ps[n] = psum.tile([P, NCOL], F32, name="lo%d" % n, tag="bank")
+            nc.tensor.matmul(out=lora_ps[n][:, c0:c1], lhsT=z_t[:, g, :], rhs=ut[n][:, c0:c1], start=True, stop=True)
 
         def lora_out(n):
             c, g = divmod(n, GROUPS)
@@ -196,125 +296,61 @@ def tile_loratacmlp4_pb_kernel(tc, h, z, u, b, W_out, b_out, out):
                 op1=ADD,
             )
 
-        def units(k):
-            if 0 <= k < n_steps:
-                return units_of[k]
-            return []
+        def finish(res, us, i0, i1):
+            c, g = divmod(us[i0], GROUPS)
+            nc.scalar.activation(out=res[:, i0:i1, :], in_=res[:, i0:i1, :], func=GELU)
+            nc.sync.dma_start(out=out_v[:, g:g + i1 - i0, NCOL * c:NCOL * c + NCOL], in_=res[:, i0:i1, :])
 
-        def plain(k):
-            blks = blocks_at.get(k, [])
-            vec = VEC_BLOCKS.get(k, ())
-            front = front_at.get(k, 0)
-            for i in range(front):
-                block(blks[i], i in vec)
-            nxt = units(k + 1)
-            nxt2 = units(k + 2)
-            tu = None
-            if nxt2:
-                tu = ps_tu.tile([P, len(nxt2), 4, P], BF16, name="tu%d" % (k + 2), tag="tu")
-            for i in range(max(len(nxt), len(nxt2))):
-                if i < len(nxt):
-                    lora_mm(nxt[i], ut[k + 1][:, i, :])
-                if i < len(nxt2):
-                    c, g = divmod(nxt2[i], GROUPS)
-                    for t in range(4):
-                        nc.tensor.transpose(tu[:, i, t, :], uraw[c][:, g, P * t:P * t + P], ident_b[:])
-            if nxt2:
-                ut[k + 2] = ut_pool.tile([P, len(nxt2), NCOL], BF16, name="ut%d" % (k + 2), tag="ut")
-                nc.scalar.copy(out=ut[k + 2][:], in_=tu[:].rearrange("q i t p -> q i (t p)"))
-            for n in nxt:
-                lora_out(n)
-            for i in range(front, len(blks)):
-                block(blks[i], i in vec)
+        def bias_mm(i, on_vector):
+            c, bb = divmod(i, 2)
+            ps = psum.tile([P, NCOL], F32, name="bias_ps%d" % i, tag="bank")
+            nc.tensor.matmul(out=ps[:], lhsT=sel[bb][:], rhs=rows[:, NCOL * c:NCOL * c + NCOL], start=True, stop=True)
+            copy_out(on_vector, bias[:, bb, NCOL * c:NCOL * c + NCOL], ps[:])
 
-        def finish(k, i0, i1):
-            c, g = divmod(units_of[k][i0], GROUPS)
-            nc.scalar.activation(out=res[k][:, i0:i1, :], in_=res[k][:, i0:i1, :], func=GELU)
-            nc.sync.dma_start(out=out_v[:, g:g + i1 - i0, NCOL * c:NCOL * c + NCOL], in_=res[k][:, i0:i1, :])
+        def z_transposes():
+            tz = psum.tile([P, GROUPS, P], BF16, name="tz", tag="bank")
+            for g in range(GROUPS):
+                nc.tensor.transpose(tz[:, g, :], zraw[:, g, :], ident_b[:])
+            nc.scalar.copy(out=z_t[:], in_=tz[:])
 
-        loads_at = {
-            0: [("h", 5), ("h", 6), ("w", 1, 2, 3)],
-            1: [("h", 7), ("w", 1, 3, 4)],
-            2: [("u", 1, 0, 8)],
-            3: [("w", 2, 0, 4)],
-            4: [("u", 2, 0, 8)],
-            5: [("w", 3, 0, 4)],
-            6: [("u", 3, 0, 8)],
-        }
+        def run(ops, us, res):
+            for op in ops:
+                if op[0] == "add":
+                    add_main(op[1], res[:, op[2], :])
+                elif op[0] == "mm":
+                    lora_mm(op[1], op[2], op[3])
+                elif op[0] == "bias":
+                    bias_mm(op[1], op[2])
+                elif op[0] == "flush":
+                    flush(op[1])
+                elif op[0] == "lout":
+                    lora_out(op[1])
+                elif op[0] == "ut":
+                    u_transposes(op[1], op[2])
+                elif op[0] == "zt":
+                    z_transposes()
+                elif op[0] == "blk":
+                    block(op[1], op[2])
+                elif op[0] == "load":
+                    do_load(op[1])
+                else:
+                    finish(res, us, op[1], op[2])
 
-        def do_load(item):
-            if item[0] == "h":
-                load_h(item[1])
-            elif item[0] == "w":
-                load_w(item[1], item[2], item[3])
-            else:
-                load_u(item[1], item[2], item[3])
-
-        warm = const.tile([P, 8], F32, name="warm")
-        nc.vector.memset(warm[:], 0.0)
-        nc.scalar.activation(out=warm[:], in_=warm[:], func=GELU)
         nc.vector.memset(rows[:].bitcast(I32), 0)
-        nc.sync.dma_start(out=rows[0:1, :], in_=bo_v)
-        nc.sync.dma_start(out=rows[32:33, :], in_=b_v[0:1, :])
-        nc.sync.dma_start(out=rows[64:65, :], in_=b_v[1:2, :])
-        nc.sync.dma_start(out=zraw[:], in_=z_v)
-        load_u(0, 0, 4)
-        load_h(0)
-        for kp in range(PASSES):
-            load_w(0, kp, kp + 1)
-        load_h(1)
-        load_h(2)
-        load_w(1, 0, 1)
-        load_h(3)
+        nc.scalar.dma_start(out=rows[0:1, :], in_=bo_v)
+        nc.scalar.dma_start(out=rows[32:33, :], in_=b_v[0:1, :])
+        nc.scalar.dma_start(out=rows[64:65, :], in_=b_v[1:2, :])
         make_identity(nc, ident_b[:])
         make_identity(nc, ident_f[:])
         for i in range(2):
             nc.vector.memset(sel[i][:], 0.0)
             nc.vector.memset(sel[i][0:1, :], 1.0)
             nc.vector.memset(sel[i][32 * (i + 1):32 * (i + 1) + 1, :], 1.0)
-
-        def bias_mm(i):
-            bb, c = divmod(i, CHUNKS)
-            if i % 2 == 0:
-                ps = ps_mm.tile([P, NCOL], F32, name="bias_ps%d" % i, tag="acc")
-            else:
-                ps = ps_lo.tile([P, NCOL], F32, name="bias_ps%d" % i, tag="lo")
-            nc.tensor.matmul(out=ps[:], lhsT=sel[bb][:], rhs=rows[:, NCOL * c:NCOL * c + NCOL], start=True, stop=True)
-            copy_out(i % 2 == 0, bias[:, bb, NCOL * c:NCOL * c + NCOL], ps[:])
-
-        for i in range(4):
-            bias_mm(i)
-        tz = ps_tu.tile([P, GROUPS, P], BF16, name="tz", tag="tu")
-        for g in range(GROUPS):
-            nc.tensor.transpose(tz[:, g, :], zraw[:, g, :], ident_b[:])
-        nc.scalar.copy(out=z_t[:], in_=tz[:])
-        plain(-2)
-        for i in range(4, 8):
-            bias_mm(i)
-        plain(-1)
-        block(("h", 0, 0, 0), True)
-        block(("h", 0, 0, 1), False)
-        for kp in range(PASSES):
-            block(("w", 0, kp, 0), True)
-            block(("w", 0, kp, 1), False)
-            flush(1)
-        load_h(4)
-        load_u(0, 4, 8)
-        load_w(1, 1, 2)
-
-        for k in range(n_steps):
-            flush(0)
-            us = units_of[k]
-            res[k] = o_pool.tile([P, len(us), NCOL], F32, name="res%d" % k, tag="res")
+        nc.vector.memset(warm[:], 0.0)
+        nc.scalar.activation(out=warm[:], in_=warm[:], func=GELU)
+        run(head, [], None)
+        for us, ops in steps:
+            res = o_pool.tile([P, len(us), NCOL], F32, name="res%d" % us[0], tag="res")
             for n in us:
                 mx(n)
-            for i in range(len(us)):
-                add_main(us[i], res[k][:, i, :])
-            plain(k)
-            for item in loads_at.get(k, []):
-                do_load(item)
-            if k == n_steps - 1:
-                for i in range(len(us)):
-                    finish(k, i, i + 1)
-            else:
-                finish(k, 0, len(us))
+            run(ops, us, res)

@@ -24,6 +24,8 @@ RANK = 128
 FLOPS = 2 * GROUPS * P * ODIM * (KDIM + RANK)
 
 LATE_STEP = 2
+FINE_STEPS = 3
+TAIL_CUTS = 2
 LEAD = 6
 VEC_BLK = {1: (0,), 3: (0,), 4: (0,)}
 W1_AT = ((1, 0, 0), (2, 0, 1), (3, 1, 0), (3, 1, 1), (4, 2, 0), (4, 2, 1), (5, 3, 0), (6, 3, 1))
@@ -96,11 +98,22 @@ def build_program():
         blks = [("blk", blk, i in vec) for i, blk in enumerate(blocks_at[k])]
         if len(us) == 1:
             ops.append(("flush", 0))
-            ops.append(("add", us[0], 0))
-        else:
-            ops.append(("add", us[0], 0))
+            ops.append(("add", us[0], 0, 0, P))
+        elif k < n_steps - FINE_STEPS:
+            ops.append(("add", us[0], 0, 0, P))
             ops.append(("flush", 0))
-            ops.append(("add", us[1], 1))
+            ops.append(("add", us[1], 1, 0, P))
+        elif k < n_steps - 1:
+            for i in range(2):
+                ops.append(("add", us[i], i, 0, P))
+                ops.append(("fin", i, i + 1, 0, NCOL))
+        else:
+            ops.append(("add", us[0], 0, 0, P))
+            ops.append(("fin", 0, 1, 0, NCOL))
+            for i in range(TAIL_CUTS):
+                w = P // TAIL_CUTS
+                ops.append(("add", us[1], 1, w * i, w * i + w))
+                ops.append(("fin", 1, 2, 4 * w * i, 4 * w * i + 4 * w))
         nxt = ahead(k + 1)
         nxt2 = ahead(k + 2)
         last = []
@@ -116,11 +129,8 @@ def build_program():
         ops.extend(last)
         for item in loads_at.get(k, []):
             ops.append(("load", item))
-        if k == n_steps - 1:
-            for i in range(len(us)):
-                ops.append(("fin", i, i + 1))
-        else:
-            ops.append(("fin", 0, len(us)))
+        if k < n_steps - FINE_STEPS:
+            ops.append(("fin", 0, len(us), 0, NCOL))
         steps.append((us, ops))
     return head, steps
 
@@ -264,8 +274,9 @@ def tile_loratacmlp4_pb_kernel(tc, h, z, u, b, W_out, b_out, out):
         def by_plane(ap):
             return ap.rearrange("q (t p) -> q p t", t=4)
 
-        def add_main(n, dst):
-            nc.vector.tensor_tensor(out=by_column(dst), in0=by_plane(main[n][:]), in1=by_column(lsum[n][:]), op=ADD)
+        def add_main(n, dst, p0, p1):
+            nc.vector.tensor_tensor(out=by_column(dst)[:, p0:p1, :], in0=by_plane(main[n][:])[:, p0:p1, :],
+                                    in1=by_column(lsum[n][:])[:, p0:p1, :], op=ADD)
 
         def u_transposes(us, tag):
             tu = psum.tile([P, len(us), 4, P], BF16, name="tu%d" % us[0], tag="bank")
@@ -296,10 +307,10 @@ def tile_loratacmlp4_pb_kernel(tc, h, z, u, b, W_out, b_out, out):
                 op1=ADD,
             )
 
-        def finish(res, us, i0, i1):
+        def finish(res, us, i0, i1, c0, c1):
             c, g = divmod(us[i0], GROUPS)
-            nc.scalar.activation(out=res[:, i0:i1, :], in_=res[:, i0:i1, :], func=GELU)
-            nc.sync.dma_start(out=out_v[:, g:g + i1 - i0, NCOL * c:NCOL * c + NCOL], in_=res[:, i0:i1, :])
+            nc.scalar.activation(out=res[:, i0:i1, c0:c1], in_=res[:, i0:i1, c0:c1], func=GELU)
+            nc.sync.dma_start(out=out_v[:, g:g + i1 - i0, NCOL * c + c0:NCOL * c + c1], in_=res[:, i0:i1, c0:c1])
 
         def bias_mm(i, on_vector):
             c, bb = divmod(i, 2)
@@ -316,7 +327,7 @@ def tile_loratacmlp4_pb_kernel(tc, h, z, u, b, W_out, b_out, out):
         def run(ops, us, res):
             for op in ops:
                 if op[0] == "add":
-                    add_main(op[1], res[:, op[2], :])
+                    add_main(op[1], res[:, op[2], :], op[3], op[4])
                 elif op[0] == "mm":
                     lora_mm(op[1], op[2], op[3])
                 elif op[0] == "bias":
@@ -334,12 +345,12 @@ def tile_loratacmlp4_pb_kernel(tc, h, z, u, b, W_out, b_out, out):
                 elif op[0] == "load":
                     do_load(op[1])
                 else:
-                    finish(res, us, op[1], op[2])
+                    finish(res, us, op[1], op[2], op[3], op[4])
 
         nc.vector.memset(rows[:].bitcast(I32), 0)
-        nc.scalar.dma_start(out=rows[0:1, :], in_=bo_v)
-        nc.scalar.dma_start(out=rows[32:33, :], in_=b_v[0:1, :])
-        nc.scalar.dma_start(out=rows[64:65, :], in_=b_v[1:2, :])
+        nc.sync.dma_start(out=rows[0:1, :], in_=bo_v)
+        nc.sync.dma_start(out=rows[32:33, :], in_=b_v[0:1, :])
+        nc.sync.dma_start(out=rows[64:65, :], in_=b_v[1:2, :])
         make_identity(nc, ident_b[:])
         make_identity(nc, ident_f[:])
         for i in range(2):

@@ -24,7 +24,7 @@ RANK = 128
 FLOPS = 2 * GROUPS * P * ODIM * (KDIM + RANK)
 
 LATE_STEP = 2
-FINE_STEPS = 3
+FINE_STEPS = 3 if LATE_STEP == 2 else 2
 TAIL_CUTS = 2
 LEAD = 6
 VEC_BLK = {1: (0,), 3: (0,), 4: (0,)}
@@ -51,9 +51,11 @@ def build_program():
         blocks_at[g - 2] = [("h", g, 0, 0), ("h", g, 0, 1)]
     for k, kp, j in W1_AT:
         blocks_at[k].append(("w", 1, kp, j))
+    per = GROUPS // LATE_STEP
     for c in (2, 3):
-        for kp in range(PASSES):
-            blocks_at[4 * c - 1 + kp].extend([("w", c, kp, 0), ("w", c, kp, 1)])
+        first = GROUPS + per * (c - 2) - 1
+        for i in range(2 * PASSES):
+            blocks_at[first + (i * per) // (2 * PASSES)].append(("w", c, i // 2, i % 2))
 
     loads_at = {
         0: [("h", 6), ("w", 1, 2, 3)],
@@ -96,41 +98,39 @@ def build_program():
         us = units_of[k]
         vec = VEC_BLK.get(k, ())
         blks = [("blk", blk, i in vec) for i, blk in enumerate(blocks_at[k])]
+        fine = k >= n_steps - FINE_STEPS
         if len(us) == 1:
             ops.append(("flush", 0))
             ops.append(("add", us[0], 0, 0, P))
-        elif k < n_steps - FINE_STEPS:
-            ops.append(("add", us[0], 0, 0, P))
-            ops.append(("flush", 0))
-            ops.append(("add", us[1], 1, 0, P))
-        elif k < n_steps - 1:
-            for i in range(2):
-                ops.append(("add", us[i], i, 0, P))
-                ops.append(("fin", i, i + 1, 0, NCOL))
         else:
-            ops.append(("add", us[0], 0, 0, P))
-            ops.append(("fin", 0, 1, 0, NCOL))
-            for i in range(TAIL_CUTS):
-                w = P // TAIL_CUTS
-                ops.append(("add", us[1], 1, w * i, w * i + w))
-                ops.append(("fin", 1, 2, 4 * w * i, 4 * w * i + 4 * w))
+            for i in range(len(us)):
+                if k == n_steps - 1 and i == len(us) - 1:
+                    w = P // TAIL_CUTS
+                    for j in range(TAIL_CUTS):
+                        ops.append(("add", us[i], i, w * j, w * j + w))
+                        ops.append(("fin", i, i + 1, 4 * w * j, 4 * w * j + 4 * w))
+                else:
+                    ops.append(("add", us[i], i, 0, P))
+                    if i == 0:
+                        ops.append(("flush", 0))
+                    if fine:
+                        ops.append(("fin", i, i + 1, 0, NCOL))
+                    elif i % 2 == 1 and i < len(us) - 1:
+                        ops.append(("fin", i - 1, i + 1, 0, NCOL))
         nxt = ahead(k + 1)
         nxt2 = ahead(k + 2)
-        last = []
-        if len(nxt) == 1:
-            ops.append(("mm", nxt[0], 0, NCOL // 2))
-            last = [("mm", nxt[0], NCOL // 2, NCOL), ("lout", nxt[0])]
-        elif len(nxt) == 2:
-            ops.extend(lora(nxt[0]))
-            last = lora(nxt[1])
         if nxt2:
-            ops.append(("ut", nxt2, "tu"))
+            ops.append(("utmm", nxt2, nxt))
+        else:
+            for n in nxt:
+                ops.append(("mm", n, 0, NCOL))
+        for n in nxt:
+            ops.append(("lout", n))
         ops.extend(blks)
-        ops.extend(last)
         for item in loads_at.get(k, []):
             ops.append(("load", item))
-        if k < n_steps - FINE_STEPS:
-            ops.append(("fin", 0, len(us), 0, NCOL))
+        if not fine:
+            ops.append(("fin", len(us) - min(2, len(us)), len(us), 0, NCOL))
         steps.append((us, ops))
     return head, steps
 
@@ -155,8 +155,8 @@ def tile_loratacmlp4_pb_kernel(tc, h, z, u, b, W_out, b_out, out):
         ut_pool = ctx.enter_context(tc.tile_pool(name="ut", bufs=3))
         grp_pool = ctx.enter_context(tc.tile_pool(name="grouped", bufs=4))
         wq_pool = ctx.enter_context(tc.tile_pool(name="wq", bufs=2))
-        l_pool = ctx.enter_context(tc.tile_pool(name="lsum", bufs=LEAD + 3))
-        o_pool = ctx.enter_context(tc.tile_pool(name="res", bufs=5))
+        l_pool = ctx.enter_context(tc.tile_pool(name="lsum", bufs=LEAD + 1 + LATE_STEP))
+        o_pool = ctx.enter_context(tc.tile_pool(name="res", bufs=(5 if LATE_STEP == 2 else 3)))
         psum = ctx.enter_context(tc.psum_pool(name="psum", bufs=8))
         ctx.enter_context(tc.manual_schedule())
 
@@ -289,6 +289,20 @@ def tile_loratacmlp4_pb_kernel(tc, h, z, u, b, W_out, b_out, out):
             for i in range(len(us)):
                 ut[us[i]] = t_sb[:, i, :]
 
+        def u_woven(us, mms):
+            tu = psum.tile([P, len(us), 4, P], BF16, name="tu%d" % us[0], tag="bank")
+            for i in range(max(len(us), len(mms))):
+                if i < len(mms):
+                    lora_mm(mms[i], 0, NCOL)
+                if i < len(us):
+                    c, g = divmod(us[i], GROUPS)
+                    for t in range(4):
+                        nc.tensor.transpose(tu[:, i, t, :], uraw[c][:, g, P * t:P * t + P], ident_b[:])
+            t_sb = ut_pool.tile([P, len(us), NCOL], BF16, name="ut%d" % us[0], tag="ut")
+            nc.scalar.copy(out=t_sb[:], in_=tu[:].rearrange("q i t p -> q i (t p)"))
+            for i in range(len(us)):
+                ut[us[i]] = t_sb[:, i, :]
+
         def lora_mm(n, c0, c1):
             g = n % GROUPS
             if c0 == 0:
@@ -338,6 +352,8 @@ def tile_loratacmlp4_pb_kernel(tc, h, z, u, b, W_out, b_out, out):
                     lora_out(op[1])
                 elif op[0] == "ut":
                     u_transposes(op[1], op[2])
+                elif op[0] == "utmm":
+                    u_woven(op[1], op[2])
                 elif op[0] == "zt":
                     z_transposes()
                 elif op[0] == "blk":
@@ -361,7 +377,8 @@ def tile_loratacmlp4_pb_kernel(tc, h, z, u, b, W_out, b_out, out):
         nc.scalar.activation(out=warm[:], in_=warm[:], func=GELU)
         run(head, [], None)
         for us, ops in steps:
-            res = o_pool.tile([P, len(us), NCOL], F32, name="res%d" % us[0], tag="res")
+            res = o_pool.tile([P, len(us), NCOL], F32, name="res%d" % us[0], tag="res%d" % len(us),
+                              bufs=(5 if len(us) < 4 else 3))
             for n in us:
                 mx(n)
             run(ops, us, res)

@@ -158,7 +158,6 @@ def tile_loratacmlp4_pb_kernel(tc, h, z, u, b, W_out, b_out, out):
         l_pool = ctx.enter_context(tc.tile_pool(name="lsum", bufs=LEAD + 1 + LATE_STEP))
         o_pool = ctx.enter_context(tc.tile_pool(name="res", bufs=(5 if LATE_STEP == 2 else 3)))
         psum = ctx.enter_context(tc.psum_pool(name="psum", bufs=8))
-        ctx.enter_context(tc.manual_schedule())
 
         hraw = {}
         wraw = {}

@@ -16,197 +16,94 @@ ADD = mybir.AluOpType.add
 P = 128
 GROUPS = 8
 CHUNKS = 4
+UNITS = GROUPS * CHUNKS
 PASSES = 4
-NCOL = 512
-KDIM = 2048
-ODIM = 2048
+CHUNK = 512
+PLANES = CHUNK // P
+IN_CH = 2048
+OUT_CH = 2048
 RANK = 128
-FLOPS = 2 * GROUPS * P * ODIM * (KDIM + RANK)
-
-LATE_STEP = 2
-FINE_STEPS = 3 if LATE_STEP == 2 else 2
-TAIL_CUTS = 2
+PASS_WORDS = 256
 LEAD = 6
-VEC_BLK = {1: (0,), 3: (0,), 4: (0,)}
-W1_AT = ((1, 0, 0), (2, 0, 1), (3, 1, 0), (3, 1, 1), (4, 2, 0), (4, 2, 1), (5, 3, 0), (6, 3, 1))
-
-
-def build_program():
-    units_of = [[g] for g in range(GROUPS)]
-    for c in range(1, CHUNKS):
-        for g in range(0, GROUPS, LATE_STEP):
-            units_of.append([GROUPS * c + g + i for i in range(LATE_STEP)])
-    n_steps = len(units_of)
-    n_units = GROUPS * CHUNKS
-
-    def ahead(k):
-        if 0 <= k < n_steps:
-            return [n + LEAD for n in units_of[k] if n + LEAD < n_units]
-        return []
-
-    blocks_at = {}
-    for k in range(n_steps):
-        blocks_at[k] = []
-    for g in range(2, GROUPS):
-        blocks_at[g - 2] = [("h", g, 0, 0), ("h", g, 0, 1)]
-    for k, kp, j in W1_AT:
-        blocks_at[k].append(("w", 1, kp, j))
-    per = GROUPS // LATE_STEP
-    for c in (2, 3):
-        first = GROUPS + per * (c - 2) - 1
-        for i in range(2 * PASSES):
-            blocks_at[first + (i * per) // (2 * PASSES)].append(("w", c, i // 2, i % 2))
-
-    loads_at = {
-        0: [("h", 6), ("w", 1, 2, 3)],
-        1: [("h", 7), ("w", 1, 3, 4)],
-        2: [("u", 2, 0, 8)],
-        3: [("w", 2, 0, 1), ("w", 2, 1, 2)],
-        4: [("w", 2, 2, 3), ("w", 2, 3, 4)],
-        5: [("u", 3, 0, 8)],
-        7: [("w", 3, 0, 1), ("w", 3, 1, 2)],
-        8: [("w", 3, 2, 3), ("w", 3, 3, 4)],
-    }
-
-    head = []
-    for item in (("z",), ("u", 0, 0, 4), ("u", 0, 4, 8), ("h", 0), ("w", 0, 0, 1), ("w", 0, 1, 2), ("w", 0, 2, 3),
-                 ("w", 0, 3, 4), ("h", 1), ("u", 1, 0, 4), ("h", 2), ("h", 3), ("w", 1, 0, 1)):
-        head.append(("load", item))
-
-    def lora(n):
-        return [("mm", n, 0, NCOL), ("lout", n)]
-
-    head.extend([("bias", 0, True), ("bias", 1, False), ("bias", 2, True), ("bias", 3, False), ("zt",)])
-    head.extend([("bias", 4, True), ("ut", [0, 1], "tu"), ("ut", [2, 3], "tu"), ("bias", 5, False)])
-    head.extend(lora(0) + lora(1) + [("ut", [4, 5], "tu")] + lora(2) + lora(3) + [("ut", [6, 7], "tu")])
-    head.extend([("blk", ("h", 0, 0, 0), False), ("blk", ("h", 0, 0, 1), False), ("load", ("h", 4))])
-    head.extend(lora(4))
-    head.extend([("blk", ("w", 0, 0, 0), False), ("blk", ("w", 0, 0, 1), False), ("flush", 1)])
-    head.extend(lora(5))
-    head.extend([("blk", ("w", 0, 1, 0), False), ("blk", ("w", 0, 1, 1), False), ("flush", 1)])
-    head.extend(lora(6))
-    head.extend([("blk", ("w", 0, 2, 0), False), ("blk", ("w", 0, 2, 1), False), ("flush", 1)])
-    head.extend([("bias", 6, True)])
-    head.extend([("blk", ("w", 0, 3, 0), True), ("blk", ("w", 0, 3, 1), False), ("flush", 0)])
-    head.extend([("bias", 7, True)])
-    head.extend([("blk", ("h", 1, 0, 0), True), ("blk", ("h", 1, 0, 1), False)])
-    head.extend([("load", ("h", 5)), ("load", ("w", 1, 1, 2)), ("load", ("u", 1, 4, 8))])
-
-    steps = []
-    for k in range(n_steps):
-        ops = []
-        us = units_of[k]
-        vec = VEC_BLK.get(k, ())
-        blks = [("blk", blk, i in vec) for i, blk in enumerate(blocks_at[k])]
-        fine = k >= n_steps - FINE_STEPS
-        if len(us) == 1:
-            ops.append(("flush", 0))
-            ops.append(("add", us[0], 0, 0, P))
-        else:
-            for i in range(len(us)):
-                if k == n_steps - 1 and i == len(us) - 1:
-                    w = P // TAIL_CUTS
-                    for j in range(TAIL_CUTS):
-                        ops.append(("add", us[i], i, w * j, w * j + w))
-                        ops.append(("fin", i, i + 1, 4 * w * j, 4 * w * j + 4 * w))
-                else:
-                    ops.append(("add", us[i], i, 0, P))
-                    if i == 0:
-                        ops.append(("flush", 0))
-                    if fine:
-                        ops.append(("fin", i, i + 1, 0, NCOL))
-                    elif i % 2 == 1 and i < len(us) - 1:
-                        ops.append(("fin", i - 1, i + 1, 0, NCOL))
-        nxt = ahead(k + 1)
-        nxt2 = ahead(k + 2)
-        if nxt2:
-            ops.append(("utmm", nxt2, nxt))
-        else:
-            for n in nxt:
-                ops.append(("mm", n, 0, NCOL))
-        for n in nxt:
-            ops.append(("lout", n))
-        ops.extend(blks)
-        for item in loads_at.get(k, []):
-            ops.append(("load", item))
-        if not fine:
-            ops.append(("fin", len(us) - min(2, len(us)), len(us), 0, NCOL))
-        steps.append((us, ops))
-    return head, steps
+FLOPS = 2 * GROUPS * P * OUT_CH * (IN_CH + RANK)
 
 
 def tile_loratacmlp4_pb_kernel(tc, h, z, u, b, W_out, b_out, out):
     nc = tc.nc
     h_v = h.rearrange("b k f c -> (b k) f c")
-    w_v = W_out.rearrange("(c p t) k -> c p t k", p=P, t=4)
-    u_v = u.rearrange("b k (c p t) r -> c p (b k) (t r)", p=P, t=4)
+    w_v = W_out.rearrange("(c p t) k -> c p t k", p=P, t=PLANES)
+    u_v = u.rearrange("b k (c p t) r -> c p (b k) (t r)", p=P, t=PLANES)
     z_v = z.rearrange("b k f r -> f (b k) r")
     b_v = b.rearrange("b x y o -> (b x y) o")
-    bo_v = b_out.rearrange("(x o) -> x o", x=1)
+    b_out_v = b_out.rearrange("(x o) -> x o", x=1)
     out_v = out.rearrange("b k f o -> f (b k) o")
 
-    head, steps = build_program()
+    steps = [[g] for g in range(GROUPS)]
+    steps += [[n, n + 1] for n in range(GROUPS, UNITS, 2)]
+    first_fine_step = len(steps) - 3
+
+    w_queue = [(c, kp, half) for c in range(1, CHUNKS) for kp in range(PASSES) for half in range(2)]
+    w_blocks_of = []
+    for k in range(len(steps)):
+        room = (3 if 1 <= k <= 6 else 2) - (2 if k + 2 < GROUPS else 0)
+        w_blocks_of.append(w_queue[:room])
+        w_queue = w_queue[room:]
+
+    def ahead(k):
+        if k >= len(steps):
+            return []
+        return [n + LEAD for n in steps[k] if n + LEAD < UNITS]
 
     with ExitStack() as ctx:
         const = ctx.enter_context(tc.tile_pool(name="const", bufs=1))
-        hraw_pool = ctx.enter_context(tc.tile_pool(name="hraw", bufs=4))
-        wraw_pool = ctx.enter_context(tc.tile_pool(name="wraw", bufs=8))
-        uraw_pool = ctx.enter_context(tc.tile_pool(name="uraw", bufs=3))
-        ut_pool = ctx.enter_context(tc.tile_pool(name="ut", bufs=3))
-        grp_pool = ctx.enter_context(tc.tile_pool(name="grouped", bufs=4))
-        wq_pool = ctx.enter_context(tc.tile_pool(name="wq", bufs=2))
-        l_pool = ctx.enter_context(tc.tile_pool(name="lsum", bufs=LEAD + 1 + LATE_STEP))
-        o_pool = ctx.enter_context(tc.tile_pool(name="res", bufs=(5 if LATE_STEP == 2 else 3)))
+        h_raw_pool = ctx.enter_context(tc.tile_pool(name="h_raw", bufs=4))
+        w_raw_pool = ctx.enter_context(tc.tile_pool(name="w_raw", bufs=2 * PASSES))
+        u_raw_pool = ctx.enter_context(tc.tile_pool(name="u_raw", bufs=3))
+        u_t_pool = ctx.enter_context(tc.tile_pool(name="u_t", bufs=3))
+        grouped_pool = ctx.enter_context(tc.tile_pool(name="grouped", bufs=4))
+        w_mx_pool = ctx.enter_context(tc.tile_pool(name="w_mx", bufs=2))
+        low_pool = ctx.enter_context(tc.tile_pool(name="low", bufs=LEAD + 3))
+        res_pool = ctx.enter_context(tc.tile_pool(name="res", bufs=5))
         psum = ctx.enter_context(tc.psum_pool(name="psum", bufs=8))
+        ctx.enter_context(tc.manual_schedule())
 
-        hraw = {}
-        wraw = {}
-        uraw = {}
-        ut = {}
-        grouped = {}
-        wcodes = {}
-        wscales = {}
-        lora_ps = {}
-        lsum = {}
-        main = {}
-        pending = []
-        done = [0]
-
-        ident_f = const.tile([P, P], F32, name="ident_f")
-        ident_b = const.tile([P, P], BF16, name="ident_b")
-        rows = const.tile([P, ODIM], BF16, name="rows")
-        sel = [const.tile([P, P], BF16, name="sel%d" % i) for i in range(2)]
-        bias = const.tile([P, 2, ODIM], F32, name="bias")
-        zraw = const.tile([P, GROUPS, RANK], BF16, name="zraw")
+        ident_f32 = const.tile([P, P], F32, name="ident_f32")
+        ident_bf16 = const.tile([P, P], BF16, name="ident_bf16")
+        bias_rows = const.tile([P, OUT_CH], BF16, name="bias_rows")
+        pick = [const.tile([P, P], BF16, name="pick%d" % i) for i in range(2)]
+        bias = const.tile([P, 2, OUT_CH], F32, name="bias")
+        z_raw = const.tile([P, GROUPS, RANK], BF16, name="z_raw")
         z_t = const.tile([P, GROUPS, P], BF16, name="z_t")
-        hcodes = const.tile([P, GROUPS, PASSES * P], U32, name="hcodes", align_bytes=64)
-        hscales = const.tile([P, GROUPS, PASSES * P], U8, name="hscales", align_bytes=64)
-        warm = const.tile([P, 8], F32, name="warm")
+        h_codes = const.tile([P, GROUPS, PASSES * P], U32, name="h_codes", align_bytes=64)
+        h_scales = const.tile([P, GROUPS, PASSES * P], U8, name="h_scales", align_bytes=64)
+        table_warmer = const.tile([P, 8], F32, name="table_warmer")
+
+        h_raw = {}
+        w_raw = {}
+        w_grouped = {}
+        w_codes = {}
+        w_scales = {}
+        u_raw = {}
+        u_t = {}
+        low_psum = {}
+        low = {}
+        copied = []
+
+        def bank(shape, dtype, name):
+            return psum.tile(shape, dtype, name=name, tag="bank")
 
         def load_h(g):
-            hraw[g] = hraw_pool.tile([P, KDIM], BF16, name="hraw%d" % g, tag="hraw")
-            nc.sync.dma_start(out=hraw[g][:], in_=h_v[g])
+            h_raw[g] = h_raw_pool.tile([P, IN_CH], BF16, name="h_raw%d" % g, tag="h_raw")
+            nc.sync.dma_start(out=h_raw[g][:], in_=h_v[g])
 
-        def load_w(c, k0, k1):
-            t = wraw_pool.tile([P, 4, 512 * (k1 - k0)], BF16, name="wraw%d_%d" % (c, k0), tag="wraw")
-            nc.sync.dma_start(out=t[:], in_=w_v[c][:, :, 512 * k0:512 * k1])
-            for kp in range(k0, k1):
-                wraw[(c, kp)] = (t, kp - k0)
+        def load_w(c, kp):
+            w_raw[(c, kp)] = w_raw_pool.tile([P, PLANES, 512], BF16, name="w_raw%d_%d" % (c, kp), tag="w_raw")
+            nc.sync.dma_start(out=w_raw[(c, kp)][:], in_=w_v[c][:, :, 512 * kp:512 * kp + 512])
 
         def load_u(c, g0, g1):
-            if c not in uraw:
-                uraw[c] = uraw_pool.tile([P, GROUPS, NCOL], BF16, name="uraw%d" % c, tag="uraw")
-            nc.sync.dma_start(out=uraw[c][:, g0:g1, :], in_=u_v[c][:, g0:g1, :])
-
-        def do_load(item):
-            if item[0] == "z":
-                nc.sync.dma_start(out=zraw[:], in_=z_v)
-            elif item[0] == "h":
-                load_h(item[1])
-            elif item[0] == "w":
-                load_w(item[1], item[2], item[3])
-            else:
-                load_u(item[1], item[2], item[3])
+            if c not in u_raw:
+                u_raw[c] = u_raw_pool.tile([P, GROUPS, CHUNK], BF16, name="u_raw%d" % c, tag="u_raw")
+            nc.sync.dma_start(out=u_raw[c][:, g0:g1, :], in_=u_v[c][:, g0:g1, :])
 
         def copy_out(on_vector, dst, src):
             if on_vector:
@@ -214,170 +111,217 @@ def tile_loratacmlp4_pb_kernel(tc, h, z, u, b, W_out, b_out, out):
             else:
                 nc.scalar.copy(out=dst, in_=src)
 
-        def block(blk, on_vector):
-            kind, a0, kp0, j = blk
-            key = (kind, a0, kp0)
-            if key not in grouped:
-                grouped[key] = grp_pool.tile([P, 4 * NCOL], BF16, name="grp_%s%d_%d" % key, tag="grp", align_bytes=64)
-            ps = psum.tile([P, 2, 2, P], F32, name="tw_%s%d_%d_%d" % blk, tag="bank")
+        def block(words_of, grouped, half, on_vector, name):
+            t_ps = bank([P, 2, 2, P], F32, name)
             for a in range(2):
                 for v in range(2):
-                    if kind == "h":
-                        w0 = 256 * (2 * j + a) + 128 * v
-                        src = hraw[a0][:].bitcast(F32)[:, w0:w0 + 128]
-                    else:
-                        wt, kl = wraw[(a0, kp0)]
-                        w0 = 256 * kl + 128 * v
-                        src = wt[:, 2 * j + a, :].bitcast(F32)[:, w0:w0 + 128]
-                    nc.tensor.transpose(ps[:, a, v, :], src, ident_f[:])
-            dst = grouped[key][:].bitcast(F32).rearrange("q (a r v) -> q a r v", a=4, v=2)
-            copy_out(on_vector, dst[:, 2 * j:2 * j + 2, :, :], ps[:].rearrange("q a v r -> q a r v"))
-            if j == 1:
-                pending.append(key)
+                    nc.tensor.transpose(t_ps[:, a, v, :], words_of(2 * half + a, v), ident_f32[:])
+            dst = grouped[:].bitcast(F32).rearrange("q (a r v) -> q a r v", a=4, v=2)
+            copy_out(on_vector, dst[:, 2 * half:2 * half + 2, :, :], t_ps[:].rearrange("q a v r -> q a r v"))
 
-        def quantise(key):
-            kind, a0, kp0 = key
-            if kind == "h":
-                codes = hcodes[:, a0, :]
-                scales = hscales[:, a0, :]
-            else:
-                if a0 not in wcodes:
-                    wcodes[a0] = wq_pool.tile([P, PASSES, NCOL], U32, name="wcodes%d" % a0, tag="wcodes", align_bytes=64)
-                    wscales[a0] = wq_pool.tile([P, PASSES, NCOL], U8, name="wscales%d" % a0, tag="wscales", align_bytes=64)
-                codes = wcodes[a0][:, kp0, :]
-                scales = wscales[a0][:, kp0, :]
-            nc.vector.quantize_mx(out=codes.bitcast(FP8X4), scales=scales, in_=grouped[key][:])
+        def h_blocks(g, first_on_vector):
+            grouped = grouped_pool.tile([P, 4 * CHUNK], BF16, name="grouped_h%d" % g, tag="grouped", align_bytes=64)
 
-        def flush(keep):
-            while len(pending) - done[0] > keep:
-                quantise(pending[done[0]])
-                done[0] = done[0] + 1
+            def words_of(kp, v):
+                w0 = PASS_WORDS * kp + P * v
+                return h_raw[g][:].bitcast(F32)[:, w0:w0 + P]
 
-        def mx(n):
+            block(words_of, grouped, 0, first_on_vector, "t_h%d_0" % g)
+            block(words_of, grouped, 1, False, "t_h%d_1" % g)
+            copied.append((grouped, h_codes[:, g, :], h_scales[:, g, :]))
+
+        def w_block(c, kp, half, on_vector):
+            if kp == 0 and half == 0:
+                w_codes[c] = w_mx_pool.tile([P, PASSES, CHUNK], U32, name="w_codes%d" % c, tag="w_codes", align_bytes=64)
+                w_scales[c] = w_mx_pool.tile([P, PASSES, CHUNK], U8, name="w_scales%d" % c, tag="w_scales",
+                                             align_bytes=64)
+            if half == 0:
+                w_grouped[(c, kp)] = grouped_pool.tile([P, 4 * CHUNK], BF16, name="grouped_w%d_%d" % (c, kp),
+                                                       tag="grouped", align_bytes=64)
+
+            def words_of(t, v):
+                return w_raw[(c, kp)][:, t, :].bitcast(F32)[:, P * v:P * v + P]
+
+            block(words_of, w_grouped[(c, kp)], half, on_vector, "t_w%d_%d_%d" % (c, kp, half))
+            if half == 1:
+                copied.append((w_grouped[(c, kp)], w_codes[c][:, kp, :], w_scales[c][:, kp, :]))
+
+        def quantise_copied(keep):
+            ready = copied[:len(copied) - keep]
+            copied[:] = copied[len(copied) - keep:]
+            for grouped, codes, scales in ready:
+                nc.vector.quantize_mx(out=codes.bitcast(FP8X4), scales=scales, in_=grouped[:])
+
+        def bias_matmul(i):
+            c, bb = divmod(i, 2)
+            cols = slice(CHUNK * c, CHUNK * c + CHUNK)
+            spread = bank([P, CHUNK], F32, "spread%d" % i)
+            nc.tensor.matmul(out=spread[:], lhsT=pick[bb][:], rhs=bias_rows[:, cols], start=True, stop=True)
+            copy_out(i % 2 == 0, bias[:, bb, cols], spread[:])
+
+        def z_transposes():
+            t_ps = bank([P, GROUPS, P], BF16, "t_z")
+            for g in range(GROUPS):
+                nc.tensor.transpose(t_ps[:, g, :], z_raw[:, g, :], ident_bf16[:])
+            nc.scalar.copy(out=z_t[:], in_=t_ps[:])
+
+        def low_matmul(n):
+            low_psum[n] = bank([P, CHUNK], F32, "low_psum%d" % n)
+            nc.tensor.matmul(out=low_psum[n][:], lhsT=z_t[:, n % GROUPS, :], rhs=u_t[n], start=True, stop=True)
+
+        def u_transposes(units, matmuls):
+            t_ps = bank([P, len(units), PLANES, P], BF16, "t_u%d" % units[0])
+            for i in range(len(units)):
+                if i < len(matmuls):
+                    low_matmul(matmuls[i])
+                c, g = divmod(units[i], GROUPS)
+                for t in range(PLANES):
+                    nc.tensor.transpose(t_ps[:, i, t, :], u_raw[c][:, g, P * t:P * t + P], ident_bf16[:])
+            t_sb = u_t_pool.tile([P, len(units), CHUNK], BF16, name="u_t%d" % units[0], tag="u_t")
+            nc.scalar.copy(out=t_sb[:], in_=t_ps[:].rearrange("q i t p -> q i (t p)"))
+            for i in range(len(units)):
+                u_t[units[i]] = t_sb[:, i, :]
+
+        def natural(ap):
+            return ap.rearrange("q (p t) -> q p t", t=PLANES)
+
+        def from_psum(ap):
+            return ap.rearrange("q (t p) -> q p t", t=PLANES)
+
+        def low_out(n):
             c, g = divmod(n, GROUPS)
-            main[n] = psum.tile([P, NCOL], F32, name="acc%d" % n, tag="bank")
-            for kp in range(PASSES):
-                nc.tensor.matmul_mx(
-                    out=main[n][:],
-                    lhsT=hcodes[:, g, P * kp:P * kp + P].bitcast(FP8X4),
-                    lhsT_scale=hscales[:, g, P * kp:P * kp + P],
-                    rhs=wcodes[c][:, kp, :].bitcast(FP8X4),
-                    rhs_scale=wscales[c][:, kp, :],
-                    start=(kp == 0),
-                    stop=(kp == PASSES - 1),
-                )
-
-        def by_column(ap):
-            return ap.rearrange("q (p t) -> q p t", t=4)
-
-        def by_plane(ap):
-            return ap.rearrange("q (t p) -> q p t", t=4)
-
-        def add_main(n, dst, p0, p1):
-            nc.vector.tensor_tensor(out=by_column(dst)[:, p0:p1, :], in0=by_plane(main[n][:])[:, p0:p1, :],
-                                    in1=by_column(lsum[n][:])[:, p0:p1, :], op=ADD)
-
-        def u_transposes(us, tag):
-            tu = psum.tile([P, len(us), 4, P], BF16, name="tu%d" % us[0], tag="bank")
-            for i in range(len(us)):
-                c, g = divmod(us[i], GROUPS)
-                for t in range(4):
-                    nc.tensor.transpose(tu[:, i, t, :], uraw[c][:, g, P * t:P * t + P], ident_b[:])
-            t_sb = ut_pool.tile([P, len(us), NCOL], BF16, name="ut%d" % us[0], tag="ut")
-            nc.scalar.copy(out=t_sb[:], in_=tu[:].rearrange("q i t p -> q i (t p)"))
-            for i in range(len(us)):
-                ut[us[i]] = t_sb[:, i, :]
-
-        def u_woven(us, mms):
-            tu = psum.tile([P, len(us), 4, P], BF16, name="tu%d" % us[0], tag="bank")
-            for i in range(max(len(us), len(mms))):
-                if i < len(mms):
-                    lora_mm(mms[i], 0, NCOL)
-                if i < len(us):
-                    c, g = divmod(us[i], GROUPS)
-                    for t in range(4):
-                        nc.tensor.transpose(tu[:, i, t, :], uraw[c][:, g, P * t:P * t + P], ident_b[:])
-            t_sb = ut_pool.tile([P, len(us), NCOL], BF16, name="ut%d" % us[0], tag="ut")
-            nc.scalar.copy(out=t_sb[:], in_=tu[:].rearrange("q i t p -> q i (t p)"))
-            for i in range(len(us)):
-                ut[us[i]] = t_sb[:, i, :]
-
-        def lora_mm(n, c0, c1):
-            g = n % GROUPS
-            if c0 == 0:
-                lora_ps[n] = psum.tile([P, NCOL], F32, name="lo%d" % n, tag="bank")
-            nc.tensor.matmul(out=lora_ps[n][:, c0:c1], lhsT=z_t[:, g, :], rhs=ut[n][:, c0:c1], start=True, stop=True)
-
-        def lora_out(n):
-            c, g = divmod(n, GROUPS)
-            lsum[n] = l_pool.tile([P, NCOL], F32, name="lsum%d" % n, tag="lsum")
+            low[n] = low_pool.tile([P, CHUNK], F32, name="low%d" % n, tag="low")
             nc.vector.scalar_tensor_tensor(
-                out=by_column(lsum[n][:]),
-                in0=by_plane(lora_ps[n][:]),
+                out=natural(low[n][:]),
+                in0=from_psum(low_psum[n][:]),
                 scalar=1.0 / RANK,
-                in1=by_column(bias[:, g // 4, NCOL * c:NCOL * c + NCOL]),
+                in1=natural(bias[:, g // 4, CHUNK * c:CHUNK * c + CHUNK]),
                 op0=MULT,
                 op1=ADD,
             )
 
-        def finish(res, us, i0, i1, c0, c1):
-            c, g = divmod(us[i0], GROUPS)
+        def mx_passes(n):
+            c, g = divmod(n, GROUPS)
+            acc = bank([P, CHUNK], F32, "acc%d" % n)
+            for kp in range(PASSES):
+                nc.tensor.matmul_mx(
+                    out=acc[:],
+                    lhsT=h_codes[:, g, P * kp:P * kp + P].bitcast(FP8X4),
+                    lhsT_scale=h_scales[:, g, P * kp:P * kp + P],
+                    rhs=w_codes[c][:, kp, :].bitcast(FP8X4),
+                    rhs_scale=w_scales[c][:, kp, :],
+                    start=(kp == 0),
+                    stop=(kp == PASSES - 1),
+                )
+            return acc
+
+        def add_low(n, acc, dst, p0, p1):
+            nc.vector.tensor_tensor(out=natural(dst)[:, p0:p1, :], in0=from_psum(acc[:])[:, p0:p1, :],
+                                    in1=natural(low[n][:])[:, p0:p1, :], op=ADD)
+
+        def gelu_and_store(res, units, i0, i1, c0, c1):
+            c, g = divmod(units[i0], GROUPS)
             nc.scalar.activation(out=res[:, i0:i1, c0:c1], in_=res[:, i0:i1, c0:c1], func=GELU)
-            nc.sync.dma_start(out=out_v[:, g:g + i1 - i0, NCOL * c + c0:NCOL * c + c1], in_=res[:, i0:i1, c0:c1])
+            nc.sync.dma_start(out=out_v[:, g:g + i1 - i0, CHUNK * c + c0:CHUNK * c + c1], in_=res[:, i0:i1, c0:c1])
 
-        def bias_mm(i, on_vector):
-            c, bb = divmod(i, 2)
-            ps = psum.tile([P, NCOL], F32, name="bias_ps%d" % i, tag="bank")
-            nc.tensor.matmul(out=ps[:], lhsT=sel[bb][:], rhs=rows[:, NCOL * c:NCOL * c + NCOL], start=True, stop=True)
-            copy_out(on_vector, bias[:, bb, NCOL * c:NCOL * c + NCOL], ps[:])
+        nc.vector.memset(bias_rows[:].bitcast(I32), 0)
+        nc.sync.dma_start(out=bias_rows[0:1, :], in_=b_out_v)
+        nc.sync.dma_start(out=bias_rows[32:33, :], in_=b_v[0:1, :])
+        nc.sync.dma_start(out=bias_rows[64:65, :], in_=b_v[1:2, :])
+        make_identity(nc, ident_bf16[:])
+        make_identity(nc, ident_f32[:])
+        for bb in range(2):
+            nc.vector.memset(pick[bb][:], 0.0)
+            nc.vector.memset(pick[bb][0:1, :], 1.0)
+            nc.vector.memset(pick[bb][32 * (bb + 1):32 * (bb + 1) + 1, :], 1.0)
+        nc.vector.memset(table_warmer[:], 0.0)
+        nc.scalar.activation(out=table_warmer[:], in_=table_warmer[:], func=GELU)
 
-        def z_transposes():
-            tz = psum.tile([P, GROUPS, P], BF16, name="tz", tag="bank")
-            for g in range(GROUPS):
-                nc.tensor.transpose(tz[:, g, :], zraw[:, g, :], ident_b[:])
-            nc.scalar.copy(out=z_t[:], in_=tz[:])
+        nc.sync.dma_start(out=z_raw[:], in_=z_v)
+        load_u(0, 0, 4)
+        load_u(0, 4, 8)
+        load_h(0)
+        for kp in range(PASSES):
+            load_w(0, kp)
+        load_h(1)
+        load_u(1, 0, 4)
+        load_h(2)
+        load_h(3)
 
-        def run(ops, us, res):
-            for op in ops:
-                if op[0] == "add":
-                    add_main(op[1], res[:, op[2], :], op[3], op[4])
-                elif op[0] == "mm":
-                    lora_mm(op[1], op[2], op[3])
-                elif op[0] == "bias":
-                    bias_mm(op[1], op[2])
-                elif op[0] == "flush":
-                    flush(op[1])
-                elif op[0] == "lout":
-                    lora_out(op[1])
-                elif op[0] == "ut":
-                    u_transposes(op[1], op[2])
-                elif op[0] == "utmm":
-                    u_woven(op[1], op[2])
-                elif op[0] == "zt":
-                    z_transposes()
-                elif op[0] == "blk":
-                    block(op[1], op[2])
-                elif op[0] == "load":
-                    do_load(op[1])
+        def h_blocks_and_loads(g, first_on_vector):
+            h_blocks(g, first_on_vector)
+            if g + 4 < GROUPS:
+                load_h(g + 4)
+                load_w(1, g)
+            if g == 1:
+                load_u(1, 4, 8)
+
+        for i in range(4):
+            bias_matmul(i)
+        z_transposes()
+        bias_matmul(4)
+        u_transposes([0, 1], [])
+        u_transposes([2, 3], [])
+        bias_matmul(5)
+        for n in (0, 2):
+            for m in (n, n + 1):
+                low_matmul(m)
+                low_out(m)
+            u_transposes([n + 4, n + 5], [])
+        h_blocks_and_loads(0, False)
+        for kp in range(PASSES):
+            if 4 + kp <= LEAD:
+                low_matmul(4 + kp)
+                low_out(4 + kp)
+            else:
+                bias_matmul(6)
+            w_block(0, kp, 0, kp == PASSES - 1)
+            w_block(0, kp, 1, False)
+            quantise_copied(1 if kp < PASSES - 1 else 0)
+        bias_matmul(7)
+        h_blocks_and_loads(1, True)
+
+        for k in range(len(steps)):
+            units = steps[k]
+            fine = k >= first_fine_step
+            res = res_pool.tile([P, len(units), CHUNK], F32, name="res%d" % units[0], tag="res%d" % len(units))
+            accs = [mx_passes(n) for n in units]
+
+            if len(units) == 1:
+                quantise_copied(0)
+                add_low(units[0], accs[0], res[:, 0, :], 0, P)
+            else:
+                add_low(units[0], accs[0], res[:, 0, :], 0, P)
+                quantise_copied(0)
+                if fine:
+                    gelu_and_store(res, units, 0, 1, 0, CHUNK)
+                if k < len(steps) - 1:
+                    add_low(units[1], accs[1], res[:, 1, :], 0, P)
+                    if fine:
+                        gelu_and_store(res, units, 1, 2, 0, CHUNK)
                 else:
-                    finish(res, us, op[1], op[2], op[3], op[4])
+                    for p0 in (0, P // 2):
+                        add_low(units[1], accs[1], res[:, 1, :], p0, p0 + P // 2)
+                        gelu_and_store(res, units, 1, 2, PLANES * p0, PLANES * p0 + CHUNK // 2)
 
-        nc.vector.memset(rows[:].bitcast(I32), 0)
-        nc.sync.dma_start(out=rows[0:1, :], in_=bo_v)
-        nc.sync.dma_start(out=rows[32:33, :], in_=b_v[0:1, :])
-        nc.sync.dma_start(out=rows[64:65, :], in_=b_v[1:2, :])
-        make_identity(nc, ident_b[:])
-        make_identity(nc, ident_f[:])
-        for i in range(2):
-            nc.vector.memset(sel[i][:], 0.0)
-            nc.vector.memset(sel[i][0:1, :], 1.0)
-            nc.vector.memset(sel[i][32 * (i + 1):32 * (i + 1) + 1, :], 1.0)
-        nc.vector.memset(warm[:], 0.0)
-        nc.scalar.activation(out=warm[:], in_=warm[:], func=GELU)
-        run(head, [], None)
-        for us, ops in steps:
-            res = o_pool.tile([P, len(us), NCOL], F32, name="res%d" % us[0], tag="res%d" % len(us),
-                              bufs=(5 if len(us) < 4 else 3))
-            for n in us:
-                mx(n)
-            run(ops, us, res)
+            matmuls = ahead(k + 1)
+            if ahead(k + 2):
+                u_transposes(ahead(k + 2), matmuls)
+            else:
+                for n in matmuls:
+                    low_matmul(n)
+            for n in matmuls:
+                low_out(n)
+            if k + 2 < GROUPS:
+                h_blocks_and_loads(k + 2, False)
+            for c, kp, half in w_blocks_of[k]:
+                w_block(c, kp, half, False)
+            if 2 <= k <= 7:
+                c, part = divmod(k - 2, 3)
+                if part == 0:
+                    load_u(c + 2, 0, GROUPS)
+                else:
+                    load_w(c + 2, 2 * part - 2)
+                    load_w(c + 2, 2 * part - 1)
+            if not fine:
+                gelu_and_store(res, units, 0, len(units), 0, CHUNK)

from contextlib import ExitStack

import concourse.mybir as mybir
from concourse.masks import make_identity

F32 = mybir.dt.float32
BF16 = mybir.dt.bfloat16
U32 = mybir.dt.uint32
U8 = mybir.dt.uint8
I32 = mybir.dt.int32
FP8X4 = mybir.dt.float8_e4m3fn_x4
GELU = mybir.ActivationFunctionType.Gelu
MULT = mybir.AluOpType.mult
ADD = mybir.AluOpType.add

P = 128
GROUPS = 8
CHUNKS = 4
UNITS = GROUPS * CHUNKS
PASSES = 4
CHUNK = 512
PLANES = CHUNK // P
IN_CH = 2048
OUT_CH = 2048
RANK = 128
PASS_WORDS = 256
LEAD = 6
FLOPS = 2 * GROUPS * P * OUT_CH * (IN_CH + RANK)


def tile_loratacmlp4_pb_kernel(tc, h, z, u, b, W_out, b_out, out):
    nc = tc.nc
    h_v = h.rearrange("b k f c -> (b k) f c")
    w_v = W_out.rearrange("(c p t) k -> c p t k", p=P, t=PLANES)
    u_v = u.rearrange("b k (c p t) r -> c p (b k) (t r)", p=P, t=PLANES)
    z_v = z.rearrange("b k f r -> f (b k) r")
    b_v = b.rearrange("b x y o -> (b x y) o")
    b_out_v = b_out.rearrange("(x o) -> x o", x=1)
    out_v = out.rearrange("b k f o -> f (b k) o")

    steps = [[g] for g in range(GROUPS)]
    steps += [[n, n + 1] for n in range(GROUPS, UNITS, 2)]
    first_fine_step = len(steps) - 3

    w_queue = [(c, kp, half) for c in range(1, CHUNKS) for kp in range(PASSES) for half in range(2)]
    w_blocks_of = []
    for k in range(len(steps)):
        room = (3 if 1 <= k <= 6 else 2) - (2 if k + 2 < GROUPS else 0)
        w_blocks_of.append(w_queue[:room])
        w_queue = w_queue[room:]

    def ahead(k):
        if k >= len(steps):
            return []
        return [n + LEAD for n in steps[k] if n + LEAD < UNITS]

    with ExitStack() as ctx:
        const = ctx.enter_context(tc.tile_pool(name="const", bufs=1))
        h_raw_pool = ctx.enter_context(tc.tile_pool(name="h_raw", bufs=4))
        w_raw_pool = ctx.enter_context(tc.tile_pool(name="w_raw", bufs=2 * PASSES))
        u_raw_pool = ctx.enter_context(tc.tile_pool(name="u_raw", bufs=3))
        u_t_pool = ctx.enter_context(tc.tile_pool(name="u_t", bufs=3))
        grouped_pool = ctx.enter_context(tc.tile_pool(name="grouped", bufs=4))
        w_mx_pool = ctx.enter_context(tc.tile_pool(name="w_mx", bufs=2))
        low_pool = ctx.enter_context(tc.tile_pool(name="low", bufs=LEAD + 3))
        res_pool = ctx.enter_context(tc.tile_pool(name="res", bufs=5))
        psum = ctx.enter_context(tc.psum_pool(name="psum", bufs=8))
        ctx.enter_context(tc.manual_schedule())

        ident_f32 = const.tile([P, P], F32, name="ident_f32")
        ident_bf16 = const.tile([P, P], BF16, name="ident_bf16")
        bias_rows = const.tile([P, OUT_CH], BF16, name="bias_rows")
        pick = [const.tile([P, P], BF16, name="pick%d" % i) for i in range(2)]
        bias = const.tile([P, 2, OUT_CH], F32, name="bias")
        z_raw = const.tile([P, GROUPS, RANK], BF16, name="z_raw")
        z_t = const.tile([P, GROUPS, P], BF16, name="z_t")
        h_codes = const.tile([P, GROUPS, PASSES * P], U32, name="h_codes", align_bytes=64)
        h_scales = const.tile([P, GROUPS, PASSES * P], U8, name="h_scales", align_bytes=64)
        table_warmer = const.tile([P, 8], F32, name="table_warmer")

        h_raw = {}
        w_raw = {}
        w_grouped = {}
        w_codes = {}
        w_scales = {}
        u_raw = {}
        u_t = {}
        low_psum = {}
        low = {}
        copied = []

        def bank(shape, dtype, name):
            return psum.tile(shape, dtype, name=name, tag="bank")

        def load_h(g):
            h_raw[g] = h_raw_pool.tile([P, IN_CH], BF16, name="h_raw%d" % g, tag="h_raw")
            nc.sync.dma_start(out=h_raw[g][:], in_=h_v[g])

        def load_w(c, kp):
            w_raw[(c, kp)] = w_raw_pool.tile([P, PLANES, 512], BF16, name="w_raw%d_%d" % (c, kp), tag="w_raw")
            nc.sync.dma_start(out=w_raw[(c, kp)][:], in_=w_v[c][:, :, 512 * kp:512 * kp + 512])

        def load_u(c, g0, g1):
            if c not in u_raw:
                u_raw[c] = u_raw_pool.tile([P, GROUPS, CHUNK], BF16, name="u_raw%d" % c, tag="u_raw")
            nc.sync.dma_start(out=u_raw[c][:, g0:g1, :], in_=u_v[c][:, g0:g1, :])

        def copy_out(on_vector, dst, src):
            if on_vector:
                nc.vector.tensor_copy(out=dst, in_=src)
            else:
                nc.scalar.copy(out=dst, in_=src)

        def block(words_of, grouped, half, on_vector, name):
            t_ps = bank([P, 2, 2, P], F32, name)
            for a in range(2):
                for v in range(2):
                    nc.tensor.transpose(t_ps[:, a, v, :], words_of(2 * half + a, v), ident_f32[:])
            dst = grouped[:].bitcast(F32).rearrange("q (a r v) -> q a r v", a=4, v=2)
            copy_out(on_vector, dst[:, 2 * half:2 * half + 2, :, :], t_ps[:].rearrange("q a v r -> q a r v"))

        def h_blocks(g, first_on_vector):
            grouped = grouped_pool.tile([P, 4 * CHUNK], BF16, name="grouped_h%d" % g, tag="grouped", align_bytes=64)

            def words_of(kp, v):
                w0 = PASS_WORDS * kp + P * v
                return h_raw[g][:].bitcast(F32)[:, w0:w0 + P]

            block(words_of, grouped, 0, first_on_vector, "t_h%d_0" % g)
            block(words_of, grouped, 1, False, "t_h%d_1" % g)
            copied.append((grouped, h_codes[:, g, :], h_scales[:, g, :]))

        def w_block(c, kp, half, on_vector):
            if kp == 0 and half == 0:
                w_codes[c] = w_mx_pool.tile([P, PASSES, CHUNK], U32, name="w_codes%d" % c, tag="w_codes", align_bytes=64)
                w_scales[c] = w_mx_pool.tile([P, PASSES, CHUNK], U8, name="w_scales%d" % c, tag="w_scales",
                                             align_bytes=64)
            if half == 0:
                w_grouped[(c, kp)] = grouped_pool.tile([P, 4 * CHUNK], BF16, name="grouped_w%d_%d" % (c, kp),
                                                       tag="grouped", align_bytes=64)

            def words_of(t, v):
                return w_raw[(c, kp)][:, t, :].bitcast(F32)[:, P * v:P * v + P]

            block(words_of, w_grouped[(c, kp)], half, on_vector, "t_w%d_%d_%d" % (c, kp, half))
            if half == 1:
                copied.append((w_grouped[(c, kp)], w_codes[c][:, kp, :], w_scales[c][:, kp, :]))

        def quantise_copied(keep):
            ready = copied[:len(copied) - keep]
            copied[:] = copied[len(copied) - keep:]
            for grouped, codes, scales in ready:
                nc.vector.quantize_mx(out=codes.bitcast(FP8X4), scales=scales, in_=grouped[:])

        def bias_matmul(i):
            c, bb = divmod(i, 2)
            cols = slice(CHUNK * c, CHUNK * c + CHUNK)
            spread = bank([P, CHUNK], F32, "spread%d" % i)
            nc.tensor.matmul(out=spread[:], lhsT=pick[bb][:], rhs=bias_rows[:, cols], start=True, stop=True)
            copy_out(i % 2 == 0, bias[:, bb, cols], spread[:])

        def z_transposes():
            t_ps = bank([P, GROUPS, P], BF16, "t_z")
            for g in range(GROUPS):
                nc.tensor.transpose(t_ps[:, g, :], z_raw[:, g, :], ident_bf16[:])
            nc.scalar.copy(out=z_t[:], in_=t_ps[:])

        def low_matmul(n):
            low_psum[n] = bank([P, CHUNK], F32, "low_psum%d" % n)
            nc.tensor.matmul(out=low_psum[n][:], lhsT=z_t[:, n % GROUPS, :], rhs=u_t[n], start=True, stop=True)

        def u_transposes(units, matmuls):
            t_ps = bank([P, len(units), PLANES, P], BF16, "t_u%d" % units[0])
            for i in range(len(units)):
                if i < len(matmuls):
                    low_matmul(matmuls[i])
                c, g = divmod(units[i], GROUPS)
                for t in range(PLANES):
                    nc.tensor.transpose(t_ps[:, i, t, :], u_raw[c][:, g, P * t:P * t + P], ident_bf16[:])
            t_sb = u_t_pool.tile([P, len(units), CHUNK], BF16, name="u_t%d" % units[0], tag="u_t")
            nc.scalar.copy(out=t_sb[:], in_=t_ps[:].rearrange("q i t p -> q i (t p)"))
            for i in range(len(units)):
                u_t[units[i]] = t_sb[:, i, :]

        def natural(ap):
            return ap.rearrange("q (p t) -> q p t", t=PLANES)

        def from_psum(ap):
            return ap.rearrange("q (t p) -> q p t", t=PLANES)

        def low_out(n):
            c, g = divmod(n, GROUPS)
            low[n] = low_pool.tile([P, CHUNK], F32, name="low%d" % n, tag="low")
            nc.vector.scalar_tensor_tensor(
                out=natural(low[n][:]),
                in0=from_psum(low_psum[n][:]),
                scalar=1.0 / RANK,
                in1=natural(bias[:, g // 4, CHUNK * c:CHUNK * c + CHUNK]),
                op0=MULT,
                op1=ADD,
            )

        def mx_passes(n):
            c, g = divmod(n, GROUPS)
            acc = bank([P, CHUNK], F32, "acc%d" % n)
            for kp in range(PASSES):
                nc.tensor.matmul_mx(
                    out=acc[:],
                    lhsT=h_codes[:, g, P * kp:P * kp + P].bitcast(FP8X4),
                    lhsT_scale=h_scales[:, g, P * kp:P * kp + P],
                    rhs=w_codes[c][:, kp, :].bitcast(FP8X4),
                    rhs_scale=w_scales[c][:, kp, :],
                    start=(kp == 0),
                    stop=(kp == PASSES - 1),
                )
            return acc

        def add_low(n, acc, dst, p0, p1):
            nc.vector.tensor_tensor(out=natural(dst)[:, p0:p1, :], in0=from_psum(acc[:])[:, p0:p1, :],
                                    in1=natural(low[n][:])[:, p0:p1, :], op=ADD)

        def gelu_and_store(res, units, i0, i1, c0, c1):
            c, g = divmod(units[i0], GROUPS)
            nc.scalar.activation(out=res[:, i0:i1, c0:c1], in_=res[:, i0:i1, c0:c1], func=GELU)
            nc.sync.dma_start(out=out_v[:, g:g + i1 - i0, CHUNK * c + c0:CHUNK * c + c1], in_=res[:, i0:i1, c0:c1])

        nc.vector.memset(bias_rows[:].bitcast(I32), 0)
        nc.sync.dma_start(out=bias_rows[0:1, :], in_=b_out_v)
        nc.sync.dma_start(out=bias_rows[32:33, :], in_=b_v[0:1, :])
        nc.sync.dma_start(out=bias_rows[64:65, :], in_=b_v[1:2, :])
        make_identity(nc, ident_bf16[:])
        make_identity(nc, ident_f32[:])
        for bb in range(2):
            nc.vector.memset(pick[bb][:], 0.0)
            nc.vector.memset(pick[bb][0:1, :], 1.0)
            nc.vector.memset(pick[bb][32 * (bb + 1):32 * (bb + 1) + 1, :], 1.0)
        nc.vector.memset(table_warmer[:], 0.0)
        nc.scalar.activation(out=table_warmer[:], in_=table_warmer[:], func=GELU)

        nc.sync.dma_start(out=z_raw[:], in_=z_v)
        load_u(0, 0, 4)
        load_u(0, 4, 8)
        load_h(0)
        for kp in range(PASSES):
            load_w(0, kp)
        load_h(1)
        load_u(1, 0, 4)
        load_h(2)
        load_h(3)

        def h_blocks_and_loads(g, first_on_vector):
            h_blocks(g, first_on_vector)
            if g + 4 < GROUPS:
                load_h(g + 4)
                load_w(1, g)
            if g == 1:
                load_u(1, 4, 8)

        for i in range(4):
            bias_matmul(i)
        z_transposes()
        bias_matmul(4)
        u_transposes([0, 1], [])
        u_transposes([2, 3], [])
        bias_matmul(5)
        for n in (0, 2):
            for m in (n, n + 1):
                low_matmul(m)
                low_out(m)
            u_transposes([n + 4, n + 5], [])
        h_blocks_and_loads(0, False)
        for kp in range(PASSES):
            if 4 + kp <= LEAD:
                low_matmul(4 + kp)
                low_out(4 + kp)
            else:
                bias_matmul(6)
            w_block(0, kp, 0, kp == PASSES - 1)
            w_block(0, kp, 1, False)
            quantise_copied(1 if kp < PASSES - 1 else 0)
        bias_matmul(7)
        h_blocks_and_loads(1, True)

        for k in range(len(steps)):
            units = steps[k]
            fine = k >= first_fine_step
            res = res_pool.tile([P, len(units), CHUNK], F32, name="res%d" % units[0], tag="res%d" % len(units))
            accs = [mx_passes(n) for n in units]

            if len(units) == 1:
                quantise_copied(0)
                add_low(units[0], accs[0], res[:, 0, :], 0, P)
            else:
                add_low(units[0], accs[0], res[:, 0, :], 0, P)
                quantise_copied(0)
                if fine:
                    gelu_and_store(res, units, 0, 1, 0, CHUNK)
                if k < len(steps) - 1:
                    add_low(units[1], accs[1], res[:, 1, :], 0, P)
                    if fine:
                        gelu_and_store(res, units, 1, 2, 0, CHUNK)
                else:
                    for p0 in (0, P // 2):
                        add_low(units[1], accs[1], res[:, 1, :], p0, p0 + P // 2)
                        gelu_and_store(res, units, 1, 2, PLANES * p0, PLANES * p0 + CHUNK // 2)

            matmuls = ahead(k + 1)
            if ahead(k + 2):
                u_transposes(ahead(k + 2), matmuls)
            else:
                for n in matmuls:
                    low_matmul(n)
            for n in matmuls:
                low_out(n)
            if k + 2 < GROUPS:
                h_blocks_and_loads(k + 2, False)
            for c, kp, half in w_blocks_of[k]:
                w_block(c, kp, half, False)
            if 2 <= k <= 7:
                c, part = divmod(k - 2, 3)
                if part == 0:
                    load_u(c + 2, 0, GROUPS)
                else:
                    load_w(c + 2, 2 * part - 2)
                    load_w(c + 2, 2 * part - 1)
            if not fine:
                gelu_and_store(res, units, 0, len(units), 0, CHUNK)
